import numpy as np
import ml_dtypes


def mxq(x, axis, fmt="e4m3"):
    dtype, down = {"e4m3": (ml_dtypes.float8_e4m3fn, 7), "e5m2": (ml_dtypes.float8_e5m2, 14)}[fmt]
    v = np.moveaxis(np.asarray(x, np.float32).astype(ml_dtypes.bfloat16).astype(np.float64), axis, -1)
    blocks = v.reshape(v.shape[:-1] + (-1, 32))
    amax = np.abs(blocks).max(-1, keepdims=True)
    byte = np.maximum(np.where(amax > 0, np.frexp(amax)[1] - 1 + 127, 0) - down, 1)
    scale = np.exp2(byte - 127.0)
    codes = (blocks / scale).astype(np.float32).astype(dtype).astype(np.float64)
    return np.moveaxis((codes * scale).reshape(v.shape), -1, axis)


WIDE = False


def mx_kscale(k):
    if not WIDE:
        return np.ones(k)
    levels = np.array([10, -10, 5, -5, 0])
    a = np.random.permutation(np.resize(levels, k // 512 * 4)).reshape(k // 512, 4)
    idx = np.arange(k)
    return np.exp2(a[idx // 512, idx % 128 // 32])


BF16 = ml_dtypes.bfloat16


def bf(x):
    return np.asarray(x, np.float32).astype(BF16)


def f64(x):
    return np.asarray(x).astype(np.float64)


S, E, H, DH = 8192, 1024, 4, 32
W = H * DH


def rotate_half(t):
    return np.stack((-t[..., 1::2], t[..., ::2]), axis=-1).reshape(t.shape)


def setup_inputs():
    s = mx_kscale(E)
    return {"hidden_states": bf(np.random.standard_normal((S, E)) * s),
            "cos": bf(np.random.uniform(size=(S, DH))),
            "sin": bf(np.random.uniform(size=(S, DH))),
            "w_qkv": bf(np.random.standard_normal((E, 3 * W)) * 2.0 / np.sqrt(E) / s[:, None]),
            "b_qkv": bf(np.random.standard_normal(3 * W) * 0.3)}


def reference(hidden_states, cos, sin, w_qkv, b_qkv):
    qkv = ((mxq(f64(hidden_states), 1, "e4m3") @ mxq(f64(w_qkv), 0, "e4m3")) + f64(b_qkv)).reshape(S, 3, H, DH)
    q, k, v = qkv[:, 0], qkv[:, 1], qkv[:, 2]
    c = f64(cos)[:, None, :]
    sn = f64(sin)[:, None, :]
    q_rot = q * c + rotate_half(q) * sn
    k_rot = k * c + rotate_half(k) * sn
    return q_rot, k_rot, v

@@ -1,0 +1,259 @@
+from contextlib import ExitStack
+
+import concourse.mybir as mybir
+from concourse.masks import make_identity
+
+F32 = mybir.dt.float32
+BF16 = mybir.dt.bfloat16
+U32 = mybir.dt.uint32
+U8 = mybir.dt.uint8
+FP8X4 = mybir.dt.float8_e4m3fn_x4
+MULT = mybir.AluOpType.mult
+ADD = mybir.AluOpType.add
+
+P = 128
+PACK = 4
+TOKENS = 8192
+HIDDEN = 1024
+HEAD_DIM = 32
+PAIRS = HEAD_DIM // 2
+QK_HEADS = 8
+QK = QK_HEADS * HEAD_DIM
+GROUP = QK // 2
+MOVING = 4 * GROUP
+PASSES = HIDDEN // (P * PACK)
+WORD_BLOCKS = HIDDEN // (2 * P)
+TILES = TOKENS // P
+ROUND = 2
+ROUNDS = TILES // ROUND
+BLOCK = 4
+TABLE_RUN = 8
+
+FLOPS = 2 * TOKENS * HIDDEN * (QK + GROUP)
+
+
+def tile_arlowvisionattention_pa_t_kernel(
+    tc, hidden_states, cos, sin, w_qkv, b_qkv, out_0, out_1, out_2
+):
+    nc = tc.nc
+    x_view = hidden_states.rearrange("(p m) k -> p m k", m=TILES)
+    out_views = [o.rearrange("(p m) h d -> p m (h d)", m=TILES) for o in (out_0, out_1, out_2)]
+
+    with ExitStack() as ctx:
+        const = ctx.enter_context(tc.tile_pool(name="const", bufs=1))
+        x_pool = ctx.enter_context(tc.tile_pool(name="x", bufs=3))
+        mx_pool = ctx.enter_context(tc.tile_pool(name="mx", bufs=3))
+        rope_pool = ctx.enter_context(tc.tile_pool(name="rope", bufs=4))
+        out_pool = ctx.enter_context(tc.tile_pool(name="out", bufs=3))
+        psum_t = ctx.enter_context(tc.psum_pool(name="psum_t", bufs=2))
+        psum_acc = ctx.enter_context(tc.psum_pool(name="psum_acc", bufs=4))
+        psum_bias = ctx.enter_context(tc.psum_pool(name="psum_bias", bufs=2))
+        ctx.enter_context(tc.manual_schedule())
+
+        x_blocks = {}
+
+        def load_block(b):
+            x_blocks[b] = x_pool.tile([P, BLOCK, HIDDEN], BF16, name="x_blk")
+            nc.sync.dma_start(out=x_blocks[b][:], in_=x_view[:, b * BLOCK : (b + 1) * BLOCK, :])
+
+        w_raw = const.tile([P, PASSES * 2, 2, QK + GROUP], BF16, name="w_raw")
+        nc.sync.dma_start(
+            out=w_raw[:], in_=w_qkv.rearrange("(gu p e) c -> p gu e c", gu=PASSES * 2, e=2)
+        )
+        load_block(0)
+        bias_all = const.tile([P, QK + GROUP], BF16, name="bias_all")
+        nc.sync.dma_start(out=bias_all[:], in_=b_qkv.partition_broadcast(P))
+        cos_sb = const.tile([P, TILES, HEAD_DIM], BF16, name="cos_sb")
+        nc.sync.dma_start(out=cos_sb[:], in_=cos.rearrange("(p m) d -> p m d", m=TILES))
+        sin_sb = const.tile([P, TILES, HEAD_DIM], BF16, name="sin_sb")
+        nc.sync.dma_start(out=sin_sb[:], in_=sin.rearrange("(p m) d -> p m d", m=TILES))
+        load_block(1)
+        load_block(2)
+
+        ident_f32 = const.tile([P, P], F32, name="ident_f32")
+        make_identity(nc, ident_f32[:])
+        ident_bf16 = const.tile([P, P], BF16, name="ident_bf16")
+        make_identity(nc, ident_bf16[:])
+
+        w_rows = w_raw[:].rearrange("p (g u) e c -> p g (u e) c", u=2)
+        w_pairs = w_rows[:, :, :, 0:QK].rearrange("p g t (n e) -> p e g n t", e=2)
+        w_even, w_odd = w_pairs[:, 0], w_pairs[:, 1]
+        w_v = w_rows[:, :, :, QK : QK + GROUP].rearrange("p g t n -> p g n t")
+        w_grouped = const.tile([P, PASSES, MOVING, PACK], BF16, name="w_grouped", align_bytes=64)
+        nc.vector.tensor_scalar(
+            out=w_grouped[:, :, 0:GROUP, :], in0=w_odd, scalar1=-1.0, scalar2=None, op0=MULT
+        )
+        nc.scalar.copy(out=w_grouped[:, :, 2 * GROUP : 3 * GROUP, :], in_=w_odd)
+        nc.vector.tensor_copy(out=w_grouped[:, :, GROUP : 2 * GROUP, :], in_=w_even)
+        nc.scalar.copy(out=w_grouped[:, :, 3 * GROUP : 4 * GROUP, :], in_=w_v)
+        w_codes = const.tile([P, PASSES, MOVING], U32, name="w_codes", align_bytes=64)
+        w_scales = const.tile([P, PASSES, MOVING], U8, name="w_scales", align_bytes=64)
+        nc.vector.quantize_mx(
+            out=w_codes[:].rearrange("p g n -> p (g n)").bitcast(FP8X4),
+            scales=w_scales[:].rearrange("p g n -> p (g n)"),
+            in_=w_grouped[:].rearrange("p g n t -> p (g n t)"),
+        )
+
+        def transpose_round(r):
+            grouped = mx_pool.tile([P, ROUND, PASSES, P, PACK], BF16, name="grouped", align_bytes=64)
+            grouped_words = grouped[:].bitcast(F32)
+            for a in range(ROUND):
+                tile_in_block = (r * ROUND + a) % BLOCK
+                words = x_blocks[r * ROUND // BLOCK][:, tile_in_block, :].bitcast(F32)
+                x_t = psum_t.tile([P, WORD_BLOCKS, P], F32, name="x_t", tag="t")
+                for j in range(WORD_BLOCKS):
+                    nc.tensor.transpose(x_t[:, j, :], words[:, j * P : (j + 1) * P], ident_f32[:])
+                nc.scalar.copy(
+                    out=grouped_words[:, a], in_=x_t[:].rearrange("p (g u) r -> p g r u", u=2)
+                )
+            return grouped
+
+        def quantise_round(grouped):
+            codes = mx_pool.tile([P, ROUND, PASSES, P], U32, name="codes", align_bytes=64)
+            scales = mx_pool.tile([P, ROUND, PASSES, P], U8, name="scales", align_bytes=64)
+            nc.vector.quantize_mx(
+                out=codes[:].rearrange("p a g r -> p (a g r)").bitcast(FP8X4),
+                scales=scales[:].rearrange("p a g r -> p (a g r)"),
+                in_=grouped[:].rearrange("p a g r t -> p (a g r t)"),
+            )
+            return codes, scales
+
+        tables_t = const.tile([P, ROUNDS, P], BF16, name="tables_t")
+
+        def transpose_tables(run):
+            first = run * TABLE_RUN * ROUND
+            mixed = rope_pool.tile([P, TABLE_RUN * ROUND, 2, HEAD_DIM], BF16, name="mixed", bufs=2)
+            nc.vector.tensor_copy(
+                out=mixed[:, :, 0, :], in_=cos_sb[:, first : first + TABLE_RUN * ROUND, :]
+            )
+            nc.vector.tensor_copy(
+                out=mixed[:, :, 1, :], in_=sin_sb[:, first : first + TABLE_RUN * ROUND, :]
+            )
+            mixed_t = psum_t.tile([P, TABLE_RUN, P], BF16, name="mixed_t", tag="t")
+            for r in range(TABLE_RUN):
+                nc.tensor.transpose(
+                    mixed_t[:, r, :],
+                    mixed[:, r * ROUND : (r + 1) * ROUND, :, :].rearrange("p a s d -> p (a s d)"),
+                    ident_bf16[:],
+                )
+            nc.scalar.copy(
+                out=tables_t[:, run * TABLE_RUN : (run + 1) * TABLE_RUN, :], in_=mixed_t[:]
+            )
+
+        def project_round(r, codes, scales):
+            accs = []
+            for a in range(ROUND):
+                acc = psum_acc.tile([P, MOVING], F32, name="acc")
+                for g in range(PASSES):
+                    nc.tensor.matmul_mx(
+                        out=acc[:],
+                        lhsT=codes[:, a, g, :].bitcast(FP8X4),
+                        lhsT_scale=scales[:, a, g, :],
+                        rhs=w_codes[:, g, :].bitcast(FP8X4),
+                        rhs_scale=w_scales[:, g, :],
+                        start=(g == 0),
+                        stop=(g == PASSES - 1),
+                    )
+                accs.append(acc)
+            bias_share = psum_bias.tile([P, ROUND, QK], F32, name="bias_share")
+            nc.tensor.matmul(
+                out=bias_share[:].rearrange("p a n -> p (a n)"),
+                lhsT=tables_t[:, r, :],
+                rhs=bias_rhs[:].rearrange("p a n -> p (a n)"),
+                start=True,
+                stop=True,
+            )
+            return accs, bias_share
+
+        def table_of(table_sb, m):
+            pairs = table_sb[:, m, :].rearrange("p (i e) -> p i e", e=2)
+            return pairs.unsqueeze(1).to_broadcast([P, QK_HEADS, PAIRS, 2])
+
+        def rope_round(r, accs, bias_share, out_blk):
+            by_cos, by_sin, summed = [], [], []
+            for a in range(ROUND):
+                m = r * ROUND + a
+                groups = accs[a][:, 0 : 3 * GROUP].rearrange("p (w h i) -> p w h i", w=3, i=PAIRS)
+                by_cos.append(rope_pool.tile([P, QK_HEADS, PAIRS, 2], F32, name="by_cos"))
+                nc.vector.tensor_tensor(
+                    out=by_cos[a][:],
+                    in0=groups[:, 1:3].rearrange("p e h i -> p h i e"),
+                    in1=table_of(cos_sb, m),
+                    op=MULT,
+                )
+                by_sin.append(rope_pool.tile([P, QK_HEADS, PAIRS, 2], F32, name="by_sin"))
+                nc.vector.tensor_tensor(
+                    out=by_sin[a][:],
+                    in0=groups[:, 0:2].rearrange("p e h i -> p h i e"),
+                    in1=table_of(sin_sb, m),
+                    op=MULT,
+                )
+                nc.vector.tensor_tensor(
+                    out=out_blk[:, 2, m % BLOCK, :],
+                    in0=accs[a][:, 3 * GROUP : 4 * GROUP],
+                    in1=bias_all[:, QK : QK + GROUP],
+                    op=ADD,
+                )
+            for a in range(ROUND):
+                summed.append(rope_pool.tile([P, QK], F32, name="summed"))
+                nc.vector.tensor_tensor(
+                    out=summed[a][:],
+                    in0=by_cos[a][:].rearrange("p h i e -> p (h i e)"),
+                    in1=bias_share[:, a, :],
+                    op=ADD,
+                )
+            for a in range(ROUND):
+                nc.gpsimd.tensor_tensor(
+                    out=out_blk[:, 0:2, (r * ROUND + a) % BLOCK, :],
+                    in0=summed[a][:].rearrange("p (j n) -> p j n", j=2),
+                    in1=by_sin[a][:].rearrange("p (j h) i e -> p j (h i e)", j=2),
+                    op=ADD,
+                )
+
+        waiting = quantise_round(transpose_round(0))
+
+        b_pairs = bias_all[:, 0:QK].rearrange("p (n e) -> p n e", e=2)
+        bias_rot = const.tile([P, QK], BF16, name="bias_rot")
+        rot_pairs = bias_rot[:].rearrange("p (n e) -> p n e", e=2)
+        nc.vector.tensor_scalar(
+            out=rot_pairs[:, :, 0], in0=b_pairs[:, :, 1], scalar1=-1.0, scalar2=None, op0=MULT
+        )
+        nc.vector.tensor_copy(out=rot_pairs[:, :, 1], in_=b_pairs[:, :, 0])
+        select = ident_bf16[:].rearrange("p (a s d) -> p a s d", a=ROUND, s=2)
+        full = [P, ROUND, QK_HEADS, HEAD_DIM]
+        bias_rhs = const.tile([P, ROUND, QK], BF16, name="bias_rhs")
+        sin_rows = const.tile([P, ROUND, QK], BF16, name="sin_rows")
+        nc.vector.tensor_tensor(
+            out=bias_rhs[:].rearrange("p a (h d) -> p a h d", d=HEAD_DIM),
+            in0=select[:, :, 0, :].unsqueeze(2).to_broadcast(full),
+            in1=bias_all[:, 0:QK].rearrange("p (h d) -> p h d", d=HEAD_DIM).unsqueeze(1).to_broadcast(full),
+            op=MULT,
+        )
+        nc.vector.tensor_tensor(
+            out=sin_rows[:].rearrange("p a (h d) -> p a h d", d=HEAD_DIM),
+            in0=select[:, :, 1, :].unsqueeze(2).to_broadcast(full),
+            in1=bias_rot[:].rearrange("p (h d) -> p h d", d=HEAD_DIM).unsqueeze(1).to_broadcast(full),
+            op=MULT,
+        )
+        nc.vector.tensor_tensor(out=bias_rhs[:], in0=bias_rhs[:], in1=sin_rows[:], op=ADD)
+        transpose_tables(0)
+
+        out_blk = None
+        for r in range(ROUNDS):
+            codes, scales = waiting
+            if r + 1 < ROUNDS:
+                if (r + 1) % TABLE_RUN == 0:
+                    transpose_tables((r + 1) // TABLE_RUN)
+                waiting = quantise_round(transpose_round(r + 1))
+            accs, bias_share = project_round(r, codes, scales)
+            if r * ROUND % BLOCK == 0:
+                out_blk = out_pool.tile([P, 3, BLOCK, GROUP], F32, name="out_blk")
+            rope_round(r, accs, bias_share, out_blk)
+            if (r + 1) * ROUND % BLOCK == 0:
+                b = r * ROUND // BLOCK
+                if b + 3 < TILES // BLOCK:
+                    load_block(b + 3)
+                for j in range(3):
+                    nc.sync.dma_start(
+                        out=out_views[j][:, b * BLOCK : (b + 1) * BLOCK, :], in_=out_blk[:, j, :, :]
+                    )

@@ -27,6 +27,8 @@ TILES = TOKENS // P
 ROUND = 2
 ROUNDS = TILES // ROUND
 BLOCK = 4
+BLOCKS = TILES // BLOCK
+X_BUFS = 3
 TABLE_RUN = 8
 
 FLOPS = 2 * TOKENS * HIDDEN * (QK + GROUP)
@@ -41,9 +43,9 @@ def tile_arlowvisionattention_pa_t_kernel(
 
     with ExitStack() as ctx:
         const = ctx.enter_context(tc.tile_pool(name="const", bufs=1))
-        x_pool = ctx.enter_context(tc.tile_pool(name="x", bufs=3))
+        x_pool = ctx.enter_context(tc.tile_pool(name="x", bufs=X_BUFS))
         mx_pool = ctx.enter_context(tc.tile_pool(name="mx", bufs=3))
-        rope_pool = ctx.enter_context(tc.tile_pool(name="rope", bufs=4))
+        rope_pool = ctx.enter_context(tc.tile_pool(name="rope", bufs=3))
         out_pool = ctx.enter_context(tc.tile_pool(name="out", bufs=3))
         psum_t = ctx.enter_context(tc.psum_pool(name="psum_t", bufs=2))
         psum_acc = ctx.enter_context(tc.psum_pool(name="psum_acc", bufs=4))
@@ -106,6 +108,8 @@ def tile_arlowvisionattention_pa_t_kernel(
                 nc.scalar.copy(
                     out=grouped_words[:, a], in_=x_t[:].rearrange("p (g u) r -> p g r u", u=2)
                 )
+            if (r + 1) * ROUND % BLOCK == 0 and r * ROUND // BLOCK + X_BUFS < BLOCKS:
+                load_block(r * ROUND // BLOCK + X_BUFS)
             return grouped
 
         def quantise_round(grouped):
@@ -140,7 +144,8 @@ def tile_arlowvisionattention_pa_t_kernel(
                 out=tables_t[:, run * TABLE_RUN : (run + 1) * TABLE_RUN, :], in_=mixed_t[:]
             )
 
-        def project_round(r, codes, scales):
+        def project_round(r, codes_and_scales):
+            codes, scales = codes_and_scales
             accs = []
             for a in range(ROUND):
                 acc = psum_acc.tile([P, MOVING], F32, name="acc")
@@ -169,21 +174,20 @@ def tile_arlowvisionattention_pa_t_kernel(
             pairs = table_sb[:, m, :].rearrange("p (i e) -> p i e", e=2)
             return pairs.unsqueeze(1).to_broadcast([P, QK_HEADS, PAIRS, 2])
 
-        def rope_round(r, accs, bias_share, out_blk):
-            by_cos, by_sin, summed = [], [], []
+        def multiply_round(r, accs, out_blk):
+            by_cos = rope_pool.tile([P, ROUND, QK_HEADS, PAIRS, 2], F32, name="by_cos")
+            by_sin = rope_pool.tile([P, ROUND, QK_HEADS, PAIRS, 2], F32, name="by_sin")
             for a in range(ROUND):
                 m = r * ROUND + a
                 groups = accs[a][:, 0 : 3 * GROUP].rearrange("p (w h i) -> p w h i", w=3, i=PAIRS)
-                by_cos.append(rope_pool.tile([P, QK_HEADS, PAIRS, 2], F32, name="by_cos"))
                 nc.vector.tensor_tensor(
-                    out=by_cos[a][:],
+                    out=by_cos[:, a],
                     in0=groups[:, 1:3].rearrange("p e h i -> p h i e"),
                     in1=table_of(cos_sb, m),
                     op=MULT,
                 )
-                by_sin.append(rope_pool.tile([P, QK_HEADS, PAIRS, 2], F32, name="by_sin"))
                 nc.vector.tensor_tensor(
-                    out=by_sin[a][:],
+                    out=by_sin[:, a],
                     in0=groups[:, 0:2].rearrange("p e h i -> p h i e"),
                     in1=table_of(sin_sb, m),
                     op=MULT,
@@ -194,23 +198,25 @@ def tile_arlowvisionattention_pa_t_kernel(
                     in1=bias_all[:, QK : QK + GROUP],
                     op=ADD,
                 )
-            for a in range(ROUND):
-                summed.append(rope_pool.tile([P, QK], F32, name="summed"))
-                nc.vector.tensor_tensor(
-                    out=summed[a][:],
-                    in0=by_cos[a][:].rearrange("p h i e -> p (h i e)"),
-                    in1=bias_share[:, a, :],
-                    op=ADD,
-                )
-            for a in range(ROUND):
-                nc.gpsimd.tensor_tensor(
-                    out=out_blk[:, 0:2, (r * ROUND + a) % BLOCK, :],
-                    in0=summed[a][:].rearrange("p (j n) -> p j n", j=2),
-                    in1=by_sin[a][:].rearrange("p (j h) i e -> p j (h i e)", j=2),
-                    op=ADD,
-                )
+            return by_cos, by_sin
 
-        waiting = quantise_round(transpose_round(0))
+        def add_round(r, by_cos, by_sin, bias_share, out_blk):
+            summed = rope_pool.tile([P, ROUND, QK], F32, name="summed")
+            nc.vector.tensor_tensor(
+                out=summed[:],
+                in0=by_cos[:].rearrange("p a h i e -> p a (h i e)"),
+                in1=bias_share[:],
+                op=ADD,
+            )
+            first = r * ROUND % BLOCK
+            nc.gpsimd.tensor_tensor(
+                out=out_blk[:, 0:2, first : first + ROUND, :],
+                in0=summed[:].rearrange("p a (j n) -> p j a n", j=2),
+                in1=by_sin[:].rearrange("p a (j h) i e -> p j a (h i e)", j=2),
+                op=ADD,
+            )
+
+        quantised = {0: quantise_round(transpose_round(0)), 1: quantise_round(transpose_round(1))}
 
         b_pairs = bias_all[:, 0:QK].rearrange("p (n e) -> p n e", e=2)
         bias_rot = const.tile([P, QK], BF16, name="bias_rot")
@@ -238,21 +244,26 @@ def tile_arlowvisionattention_pa_t_kernel(
         nc.vector.tensor_tensor(out=bias_rhs[:], in0=bias_rhs[:], in1=sin_rows[:], op=ADD)
         transpose_tables(0)
 
+        products = {0: project_round(0, quantised[0])}
+
         out_blk = None
         for r in range(ROUNDS):
-            codes, scales = waiting
+            grouped = None
+            if r + 2 < ROUNDS:
+                if (r + 2) % TABLE_RUN == 0:
+                    transpose_tables((r + 2) // TABLE_RUN)
+                grouped = transpose_round(r + 2)
             if r + 1 < ROUNDS:
-                if (r + 1) % TABLE_RUN == 0:
-                    transpose_tables((r + 1) // TABLE_RUN)
-                waiting = quantise_round(transpose_round(r + 1))
-            accs, bias_share = project_round(r, codes, scales)
+                products[r + 1] = project_round(r + 1, quantised[r + 1])
+            accs, bias_share = products[r]
             if r * ROUND % BLOCK == 0:
                 out_blk = out_pool.tile([P, 3, BLOCK, GROUP], F32, name="out_blk")
-            rope_round(r, accs, bias_share, out_blk)
+            by_cos, by_sin = multiply_round(r, accs, out_blk)
+            if r + 2 < ROUNDS:
+                quantised[r + 2] = quantise_round(grouped)
+            add_round(r, by_cos, by_sin, bias_share, out_blk)
             if (r + 1) * ROUND % BLOCK == 0:
                 b = r * ROUND // BLOCK
-                if b + 3 < TILES // BLOCK:
-                    load_block(b + 3)
                 for j in range(3):
                     nc.sync.dma_start(
                         out=out_views[j][:, b * BLOCK : (b + 1) * BLOCK, :], in_=out_blk[:, j, :, :]

@@ -54,28 +54,76 @@ def tile_arlowvisionattention_pa_t_kernel(
 
         x_blocks = {}
 
-        def load_block(b):
+        def load_block(b, pieces):
             x_blocks[b] = x_pool.tile([P, BLOCK, HIDDEN], BF16, name="x_blk")
-            nc.sync.dma_start(out=x_blocks[b][:], in_=x_view[:, b * BLOCK : (b + 1) * BLOCK, :])
+            step = BLOCK // pieces
+            for first in range(0, BLOCK, step):
+                nc.sync.dma_start(
+                    out=x_blocks[b][:, first : first + step, :],
+                    in_=x_view[:, b * BLOCK + first : b * BLOCK + first + step, :],
+                )
 
+        cos_sb = const.tile([P, TILES, HEAD_DIM], BF16, name="cos_sb")
+        sin_sb = const.tile([P, TILES, HEAD_DIM], BF16, name="sin_sb")
+
+        def load_tables(first, last):
+            for table_sb, table in ((cos_sb, cos), (sin_sb, sin)):
+                nc.sync.dma_start(
+                    out=table_sb[:, first:last, :],
+                    in_=table.rearrange("(p m) d -> p m d", m=TILES)[:, first:last, :],
+                )
+
+        bias_row = const.tile([P, MOVING], BF16, name="bias_row")
+        nc.vector.memset(bias_row[:], 0.0)
+        nc.sync.dma_start(
+            out=bias_row[0:1, 0 : QK + GROUP], in_=b_qkv.rearrange("(o n) -> o n", o=1)
+        )
         w_raw = const.tile([P, PASSES * 2, 2, QK + GROUP], BF16, name="w_raw")
         nc.sync.dma_start(
             out=w_raw[:], in_=w_qkv.rearrange("(gu p e) c -> p gu e c", gu=PASSES * 2, e=2)
         )
-        load_block(0)
-        bias_all = const.tile([P, QK + GROUP], BF16, name="bias_all")
-        nc.sync.dma_start(out=bias_all[:], in_=b_qkv.partition_broadcast(P))
-        cos_sb = const.tile([P, TILES, HEAD_DIM], BF16, name="cos_sb")
-        nc.sync.dma_start(out=cos_sb[:], in_=cos.rearrange("(p m) d -> p m d", m=TILES))
-        sin_sb = const.tile([P, TILES, HEAD_DIM], BF16, name="sin_sb")
-        nc.sync.dma_start(out=sin_sb[:], in_=sin.rearrange("(p m) d -> p m d", m=TILES))
-        load_block(1)
-        load_block(2)
+        load_block(0, BLOCK // ROUND)
+        load_tables(0, TABLE_RUN * ROUND)
+        for b in range(1, X_BUFS):
+            load_block(b, 1)
+        load_tables(TABLE_RUN * ROUND, TILES)
 
         ident_f32 = const.tile([P, P], F32, name="ident_f32")
         make_identity(nc, ident_f32[:])
         ident_bf16 = const.tile([P, P], BF16, name="ident_bf16")
         make_identity(nc, ident_bf16[:])
+
+        ones = const.tile([P, P], BF16, name="ones")
+        nc.vector.memset(ones[:], 1.0)
+        bias_spread = psum_acc.tile([P, MOVING], F32, name="bias_spread", tag="acc")
+        nc.tensor.matmul(out=bias_spread[:], lhsT=ones[:], rhs=bias_row[:], start=True, stop=True)
+        bias_all = const.tile([P, QK + GROUP], BF16, name="bias_all")
+        nc.scalar.copy(out=bias_all[:], in_=bias_spread[:, 0 : QK + GROUP])
+
+        b_pairs = bias_all[:, 0:QK].rearrange("p (n e) -> p n e", e=2)
+        bias_rot = const.tile([P, QK], BF16, name="bias_rot")
+        rot_pairs = bias_rot[:].rearrange("p (n e) -> p n e", e=2)
+        nc.vector.tensor_scalar(
+            out=rot_pairs[:, :, 0], in0=b_pairs[:, :, 1], scalar1=-1.0, scalar2=None, op0=MULT
+        )
+        nc.vector.tensor_copy(out=rot_pairs[:, :, 1], in_=b_pairs[:, :, 0])
+        select = ident_bf16[:].rearrange("p (a s d) -> p a s d", a=ROUND, s=2)
+        full = [P, ROUND, QK_HEADS, HEAD_DIM]
+        bias_rhs = const.tile([P, ROUND, QK], BF16, name="bias_rhs")
+        sin_rows = const.tile([P, ROUND, QK], BF16, name="sin_rows")
+        nc.vector.tensor_tensor(
+            out=bias_rhs[:].rearrange("p a (h d) -> p a h d", d=HEAD_DIM),
+            in0=select[:, :, 0, :].unsqueeze(2).to_broadcast(full),
+            in1=bias_all[:, 0:QK].rearrange("p (h d) -> p h d", d=HEAD_DIM).unsqueeze(1).to_broadcast(full),
+            op=MULT,
+        )
+        nc.vector.tensor_tensor(
+            out=sin_rows[:].rearrange("p a (h d) -> p a h d", d=HEAD_DIM),
+            in0=select[:, :, 1, :].unsqueeze(2).to_broadcast(full),
+            in1=bias_rot[:].rearrange("p (h d) -> p h d", d=HEAD_DIM).unsqueeze(1).to_broadcast(full),
+            op=MULT,
+        )
+        nc.vector.tensor_tensor(out=bias_rhs[:], in0=bias_rhs[:], in1=sin_rows[:], op=ADD)
 
         w_rows = w_raw[:].rearrange("p (g u) e c -> p g (u e) c", u=2)
         w_pairs = w_rows[:, :, :, 0:QK].rearrange("p g t (n e) -> p e g n t", e=2)
@@ -109,7 +157,7 @@ def tile_arlowvisionattention_pa_t_kernel(
                     out=grouped_words[:, a], in_=x_t[:].rearrange("p (g u) r -> p g r u", u=2)
                 )
             if (r + 1) * ROUND % BLOCK == 0 and r * ROUND // BLOCK + X_BUFS < BLOCKS:
-                load_block(r * ROUND // BLOCK + X_BUFS)
+                load_block(r * ROUND // BLOCK + X_BUFS, 1)
             return grouped
 
         def quantise_round(grouped):
@@ -148,7 +196,7 @@ def tile_arlowvisionattention_pa_t_kernel(
             codes, scales = codes_and_scales
             accs = []
             for a in range(ROUND):
-                acc = psum_acc.tile([P, MOVING], F32, name="acc")
+                acc = psum_acc.tile([P, MOVING], F32, name="acc", tag="acc")
                 for g in range(PASSES):
                     nc.tensor.matmul_mx(
                         out=acc[:],
@@ -216,55 +264,29 @@ def tile_arlowvisionattention_pa_t_kernel(
                 op=ADD,
             )
 
-        quantised = {0: quantise_round(transpose_round(0)), 1: quantise_round(transpose_round(1))}
-
-        b_pairs = bias_all[:, 0:QK].rearrange("p (n e) -> p n e", e=2)
-        bias_rot = const.tile([P, QK], BF16, name="bias_rot")
-        rot_pairs = bias_rot[:].rearrange("p (n e) -> p n e", e=2)
-        nc.vector.tensor_scalar(
-            out=rot_pairs[:, :, 0], in0=b_pairs[:, :, 1], scalar1=-1.0, scalar2=None, op0=MULT
-        )
-        nc.vector.tensor_copy(out=rot_pairs[:, :, 1], in_=b_pairs[:, :, 0])
-        select = ident_bf16[:].rearrange("p (a s d) -> p a s d", a=ROUND, s=2)
-        full = [P, ROUND, QK_HEADS, HEAD_DIM]
-        bias_rhs = const.tile([P, ROUND, QK], BF16, name="bias_rhs")
-        sin_rows = const.tile([P, ROUND, QK], BF16, name="sin_rows")
-        nc.vector.tensor_tensor(
-            out=bias_rhs[:].rearrange("p a (h d) -> p a h d", d=HEAD_DIM),
-            in0=select[:, :, 0, :].unsqueeze(2).to_broadcast(full),
-            in1=bias_all[:, 0:QK].rearrange("p (h d) -> p h d", d=HEAD_DIM).unsqueeze(1).to_broadcast(full),
-            op=MULT,
-        )
-        nc.vector.tensor_tensor(
-            out=sin_rows[:].rearrange("p a (h d) -> p a h d", d=HEAD_DIM),
-            in0=select[:, :, 1, :].unsqueeze(2).to_broadcast(full),
-            in1=bias_rot[:].rearrange("p (h d) -> p h d", d=HEAD_DIM).unsqueeze(1).to_broadcast(full),
-            op=MULT,
-        )
-        nc.vector.tensor_tensor(out=bias_rhs[:], in0=bias_rhs[:], in1=sin_rows[:], op=ADD)
-        transpose_tables(0)
-
-        products = {0: project_round(0, quantised[0])}
-
+        quantised, products = {}, {}
         out_blk = None
-        for r in range(ROUNDS):
+        for r in range(-2, ROUNDS):
             grouped = None
             if r + 2 < ROUNDS:
+                grouped = transpose_round(r + 2)
                 if (r + 2) % TABLE_RUN == 0:
                     transpose_tables((r + 2) // TABLE_RUN)
-                grouped = transpose_round(r + 2)
-            if r + 1 < ROUNDS:
+            if 0 <= r + 1 < ROUNDS:
                 products[r + 1] = project_round(r + 1, quantised[r + 1])
-            accs, bias_share = products[r]
-            if r * ROUND % BLOCK == 0:
-                out_blk = out_pool.tile([P, 3, BLOCK, GROUP], F32, name="out_blk")
-            by_cos, by_sin = multiply_round(r, accs, out_blk)
+            if r >= 0:
+                accs, bias_share = products[r]
+                if r * ROUND % BLOCK == 0:
+                    out_blk = out_pool.tile([P, 3, BLOCK, GROUP], F32, name="out_blk")
+                by_cos, by_sin = multiply_round(r, accs, out_blk)
             if r + 2 < ROUNDS:
                 quantised[r + 2] = quantise_round(grouped)
-            add_round(r, by_cos, by_sin, bias_share, out_blk)
-            if (r + 1) * ROUND % BLOCK == 0:
-                b = r * ROUND // BLOCK
-                for j in range(3):
-                    nc.sync.dma_start(
-                        out=out_views[j][:, b * BLOCK : (b + 1) * BLOCK, :], in_=out_blk[:, j, :, :]
-                    )
+            if r >= 0:
+                add_round(r, by_cos, by_sin, bias_share, out_blk)
+                if (r + 1) * ROUND % BLOCK == 0:
+                    b = r * ROUND // BLOCK
+                    for j in range(3):
+                        nc.sync.dma_start(
+                            out=out_views[j][:, b * BLOCK : (b + 1) * BLOCK, :],
+                            in_=out_blk[:, j, :, :],
+                        )

@@ -222,7 +222,14 @@ def tile_arlowvisionattention_pa_t_kernel(
             pairs = table_sb[:, m, :].rearrange("p (i e) -> p i e", e=2)
             return pairs.unsqueeze(1).to_broadcast([P, QK_HEADS, PAIRS, 2])
 
-        def multiply_round(r, accs, out_blk):
+        def copy_v_round(r, accs, out_blk):
+            for a in range(ROUND):
+                nc.scalar.copy(
+                    out=out_blk[:, 2, (r * ROUND + a) % BLOCK, :],
+                    in_=accs[a][:, 3 * GROUP : 4 * GROUP],
+                )
+
+        def multiply_round(r, accs):
             by_cos = rope_pool.tile([P, ROUND, QK_HEADS, PAIRS, 2], F32, name="by_cos")
             by_sin = rope_pool.tile([P, ROUND, QK_HEADS, PAIRS, 2], F32, name="by_sin")
             for a in range(ROUND):
@@ -240,15 +247,9 @@ def tile_arlowvisionattention_pa_t_kernel(
                     in1=table_of(sin_sb, m),
                     op=MULT,
                 )
-                nc.vector.tensor_tensor(
-                    out=out_blk[:, 2, m % BLOCK, :],
-                    in0=accs[a][:, 3 * GROUP : 4 * GROUP],
-                    in1=bias_all[:, QK : QK + GROUP],
-                    op=ADD,
-                )
             return by_cos, by_sin
 
-        def add_round(r, by_cos, by_sin, bias_share, out_blk):
+        def add_bias_share(by_cos, bias_share):
             summed = rope_pool.tile([P, ROUND, QK], F32, name="summed")
             nc.vector.tensor_tensor(
                 out=summed[:],
@@ -256,6 +257,9 @@ def tile_arlowvisionattention_pa_t_kernel(
                 in1=bias_share[:],
                 op=ADD,
             )
+            return summed
+
+        def finish_qk_round(r, summed, by_sin, out_blk):
             first = r * ROUND % BLOCK
             nc.gpsimd.tensor_tensor(
                 out=out_blk[:, 0:2, first : first + ROUND, :],
@@ -264,8 +268,13 @@ def tile_arlowvisionattention_pa_t_kernel(
                 op=ADD,
             )
 
-        quantised, products = {}, {}
-        out_blk = None
+        def finish_v_round(r, out_blk):
+            first = r * ROUND % BLOCK
+            v_rows = out_blk[:, 2, first : first + ROUND, :]
+            bias_v = bias_all[:, QK : QK + GROUP].unsqueeze(1).to_broadcast([P, ROUND, GROUP])
+            nc.gpsimd.tensor_tensor(out=v_rows, in0=v_rows, in1=bias_v, op=ADD)
+
+        quantised, products, out_blks = {}, {}, {}
         for r in range(-2, ROUNDS):
             grouped = None
             if r + 2 < ROUNDS:
@@ -274,19 +283,25 @@ def tile_arlowvisionattention_pa_t_kernel(
                     transpose_tables((r + 2) // TABLE_RUN)
             if 0 <= r + 1 < ROUNDS:
                 products[r + 1] = project_round(r + 1, quantised[r + 1])
+                if (r + 1) * ROUND % BLOCK == 0:
+                    out_blks[(r + 1) * ROUND // BLOCK] = out_pool.tile(
+                        [P, 3, BLOCK, GROUP], F32, name="out_blk"
+                    )
+                copy_v_round(r + 1, products[r + 1][0], out_blks[(r + 1) * ROUND // BLOCK])
             if r >= 0:
                 accs, bias_share = products[r]
-                if r * ROUND % BLOCK == 0:
-                    out_blk = out_pool.tile([P, 3, BLOCK, GROUP], F32, name="out_blk")
-                by_cos, by_sin = multiply_round(r, accs, out_blk)
+                by_cos, by_sin = multiply_round(r, accs)
+                summed = add_bias_share(by_cos, bias_share)
             if r + 2 < ROUNDS:
                 quantised[r + 2] = quantise_round(grouped)
             if r >= 0:
-                add_round(r, by_cos, by_sin, bias_share, out_blk)
-                if (r + 1) * ROUND % BLOCK == 0:
-                    b = r * ROUND // BLOCK
-                    for j in range(3):
-                        nc.sync.dma_start(
-                            out=out_views[j][:, b * BLOCK : (b + 1) * BLOCK, :],
-                            in_=out_blk[:, j, :, :],
-                        )
+                finish_qk_round(r, summed, by_sin, out_blks[r * ROUND // BLOCK])
+            if 0 <= r + 1 < ROUNDS:
+                finish_v_round(r + 1, out_blks[(r + 1) * ROUND // BLOCK])
+            if r >= 0 and (r + 1) * ROUND % BLOCK == 0:
+                b = r * ROUND // BLOCK
+                for j in range(3):
+                    nc.sync.dma_start(
+                        out=out_views[j][:, b * BLOCK : (b + 1) * BLOCK, :],
+                        in_=out_blks[b][:, j, :, :],
+                    )

@@ -10,6 +10,7 @@ U8 = mybir.dt.uint8
 FP8X4 = mybir.dt.float8_e4m3fn_x4
 MULT = mybir.AluOpType.mult
 ADD = mybir.AluOpType.add
+IDENTITY = mybir.ActivationFunctionType.Identity
 
 P = 128
 PACK = 4
@@ -19,8 +20,7 @@ HEAD_DIM = 32
 PAIRS = HEAD_DIM // 2
 QK_HEADS = 8
 QK = QK_HEADS * HEAD_DIM
-GROUP = QK // 2
-MOVING = 4 * GROUP
+V = 4 * HEAD_DIM
 PASSES = HIDDEN // (P * PACK)
 WORD_BLOCKS = HIDDEN // (2 * P)
 TILES = TOKENS // P
@@ -31,7 +31,7 @@ BLOCKS = TILES // BLOCK
 X_BUFS = 3
 TABLE_RUN = 8
 
-FLOPS = 2 * TOKENS * HIDDEN * (QK + GROUP)
+FLOPS = 2 * TOKENS * HIDDEN * (QK + V)
 
 
 def tile_arlowvisionattention_pa_t_kernel(
@@ -46,10 +46,12 @@ def tile_arlowvisionattention_pa_t_kernel(
         x_pool = ctx.enter_context(tc.tile_pool(name="x", bufs=X_BUFS))
         mx_pool = ctx.enter_context(tc.tile_pool(name="mx", bufs=3))
         rope_pool = ctx.enter_context(tc.tile_pool(name="rope", bufs=3))
+        table_pool = ctx.enter_context(tc.tile_pool(name="table", bufs=2))
         out_pool = ctx.enter_context(tc.tile_pool(name="out", bufs=3))
         psum_t = ctx.enter_context(tc.psum_pool(name="psum_t", bufs=2))
-        psum_acc = ctx.enter_context(tc.psum_pool(name="psum_acc", bufs=4))
+        psum_qk = ctx.enter_context(tc.psum_pool(name="psum_qk", bufs=2))
         psum_bias = ctx.enter_context(tc.psum_pool(name="psum_bias", bufs=2))
+        psum_v = ctx.enter_context(tc.psum_pool(name="psum_v", bufs=1))
         ctx.enter_context(tc.manual_schedule())
 
         x_blocks = {}
@@ -73,12 +75,10 @@ def tile_arlowvisionattention_pa_t_kernel(
                     in_=table.rearrange("(p m) d -> p m d", m=TILES)[:, first:last, :],
                 )
 
-        bias_row = const.tile([P, MOVING], BF16, name="bias_row")
+        bias_row = const.tile([P, QK + V], BF16, name="bias_row")
         nc.vector.memset(bias_row[:], 0.0)
-        nc.sync.dma_start(
-            out=bias_row[0:1, 0 : QK + GROUP], in_=b_qkv.rearrange("(o n) -> o n", o=1)
-        )
-        w_raw = const.tile([P, PASSES * 2, 2, QK + GROUP], BF16, name="w_raw")
+        nc.sync.dma_start(out=bias_row[0:1, :], in_=b_qkv.rearrange("(o n) -> o n", o=1))
+        w_raw = const.tile([P, PASSES * 2, 2, QK + V], BF16, name="w_raw")
         nc.sync.dma_start(
             out=w_raw[:], in_=w_qkv.rearrange("(gu p e) c -> p gu e c", gu=PASSES * 2, e=2)
         )
@@ -95,57 +95,66 @@ def tile_arlowvisionattention_pa_t_kernel(
 
         ones = const.tile([P, P], BF16, name="ones")
         nc.vector.memset(ones[:], 1.0)
-        bias_spread = psum_acc.tile([P, MOVING], F32, name="bias_spread", tag="acc")
-        nc.tensor.matmul(out=bias_spread[:], lhsT=ones[:], rhs=bias_row[:], start=True, stop=True)
-        bias_all = const.tile([P, QK + GROUP], BF16, name="bias_all")
-        nc.scalar.copy(out=bias_all[:], in_=bias_spread[:, 0 : QK + GROUP])
-
-        b_pairs = bias_all[:, 0:QK].rearrange("p (n e) -> p n e", e=2)
-        bias_rot = const.tile([P, QK], BF16, name="bias_rot")
-        rot_pairs = bias_rot[:].rearrange("p (n e) -> p n e", e=2)
-        nc.vector.tensor_scalar(
-            out=rot_pairs[:, :, 0], in0=b_pairs[:, :, 1], scalar1=-1.0, scalar2=None, op0=MULT
+        bias_spread = psum_qk.tile([P, QK], F32, name="bias_spread", tag="qk")
+        nc.tensor.matmul(
+            out=bias_spread[:], lhsT=ones[:], rhs=bias_row[:, 0:QK], start=True, stop=True
         )
-        nc.vector.tensor_copy(out=rot_pairs[:, :, 1], in_=b_pairs[:, :, 0])
+        bias_qk = const.tile([P, QK], BF16, name="bias_qk")
+        nc.scalar.copy(out=bias_qk[:], in_=bias_spread[:])
+        bias_row_t = psum_t.tile([P, P], BF16, name="bias_row_t", tag="t")
+        nc.tensor.transpose(bias_row_t[:], bias_row[:, QK : QK + V], ident_bf16[:])
+        bias_v = const.tile([P, 1], F32, name="bias_v")
+        nc.scalar.copy(out=bias_v[:], in_=bias_row_t[:, 0:1])
+
+        bias_swap = const.tile([P, QK], BF16, name="bias_swap")
+        nc.vector.tensor_copy(
+            out=bias_swap[:].rearrange("p (n e) -> p n e", e=2),
+            in_=bias_qk[:].rearrange("p (n e) -> p n e", e=2)[:, :, ::-1],
+        )
         select = ident_bf16[:].rearrange("p (a s d) -> p a s d", a=ROUND, s=2)
         full = [P, ROUND, QK_HEADS, HEAD_DIM]
         bias_rhs = const.tile([P, ROUND, QK], BF16, name="bias_rhs")
         sin_rows = const.tile([P, ROUND, QK], BF16, name="sin_rows")
-        nc.vector.tensor_tensor(
-            out=bias_rhs[:].rearrange("p a (h d) -> p a h d", d=HEAD_DIM),
-            in0=select[:, :, 0, :].unsqueeze(2).to_broadcast(full),
-            in1=bias_all[:, 0:QK].rearrange("p (h d) -> p h d", d=HEAD_DIM).unsqueeze(1).to_broadcast(full),
-            op=MULT,
-        )
-        nc.vector.tensor_tensor(
-            out=sin_rows[:].rearrange("p a (h d) -> p a h d", d=HEAD_DIM),
-            in0=select[:, :, 1, :].unsqueeze(2).to_broadcast(full),
-            in1=bias_rot[:].rearrange("p (h d) -> p h d", d=HEAD_DIM).unsqueeze(1).to_broadcast(full),
-            op=MULT,
-        )
+        for rows, s, bias in ((bias_rhs, 0, bias_qk), (sin_rows, 1, bias_swap)):
+            nc.vector.tensor_tensor(
+                out=rows[:].rearrange("p a (h d) -> p a h d", d=HEAD_DIM),
+                in0=select[:, :, s, :].unsqueeze(2).to_broadcast(full),
+                in1=bias[:].rearrange("p (h d) -> p h d", d=HEAD_DIM).unsqueeze(1).to_broadcast(full),
+                op=MULT,
+            )
         nc.vector.tensor_tensor(out=bias_rhs[:], in0=bias_rhs[:], in1=sin_rows[:], op=ADD)
+        signs = const.tile([P, HEAD_DIM], BF16, name="signs")
+        nc.vector.memset(signs[:], 1.0)
+        nc.vector.memset(signs[:].rearrange("p (i e) -> p i e", e=2)[:, :, 0], -1.0)
 
         w_rows = w_raw[:].rearrange("p (g u) e c -> p g (u e) c", u=2)
-        w_pairs = w_rows[:, :, :, 0:QK].rearrange("p g t (n e) -> p e g n t", e=2)
-        w_even, w_odd = w_pairs[:, 0], w_pairs[:, 1]
-        w_v = w_rows[:, :, :, QK : QK + GROUP].rearrange("p g t n -> p g n t")
-        w_grouped = const.tile([P, PASSES, MOVING, PACK], BF16, name="w_grouped", align_bytes=64)
-        nc.vector.tensor_scalar(
-            out=w_grouped[:, :, 0:GROUP, :], in0=w_odd, scalar1=-1.0, scalar2=None, op0=MULT
+        w_halves = w_rows[:, :, :, 0:QK].rearrange("p g t (n e) -> p e g n t", e=2)
+        w_qk_grouped = const.tile(
+            [P, PASSES, 2, QK // 2, PACK], BF16, name="w_qk_grouped", align_bytes=64
         )
-        nc.scalar.copy(out=w_grouped[:, :, 2 * GROUP : 3 * GROUP, :], in_=w_odd)
-        nc.vector.tensor_copy(out=w_grouped[:, :, GROUP : 2 * GROUP, :], in_=w_even)
-        nc.scalar.copy(out=w_grouped[:, :, 3 * GROUP : 4 * GROUP, :], in_=w_v)
-        w_codes = const.tile([P, PASSES, MOVING], U32, name="w_codes", align_bytes=64)
-        w_scales = const.tile([P, PASSES, MOVING], U8, name="w_scales", align_bytes=64)
+        nc.vector.tensor_copy(out=w_qk_grouped[:, :, 0], in_=w_halves[:, 0])
+        nc.scalar.copy(out=w_qk_grouped[:, :, 1], in_=w_halves[:, 1])
+        w_v_grouped = const.tile([P, PASSES, V, PACK], BF16, name="w_v_grouped", align_bytes=64)
+        nc.vector.tensor_copy(
+            out=w_v_grouped[:], in_=w_rows[:, :, :, QK : QK + V].rearrange("p g t n -> p g n t")
+        )
+        w_qk_codes = const.tile([P, PASSES, QK], U32, name="w_qk_codes", align_bytes=64)
+        w_qk_scales = const.tile([P, PASSES, QK], U8, name="w_qk_scales", align_bytes=64)
         nc.vector.quantize_mx(
-            out=w_codes[:].rearrange("p g n -> p (g n)").bitcast(FP8X4),
-            scales=w_scales[:].rearrange("p g n -> p (g n)"),
-            in_=w_grouped[:].rearrange("p g n t -> p (g n t)"),
+            out=w_qk_codes[:].rearrange("p g n -> p (g n)").bitcast(FP8X4),
+            scales=w_qk_scales[:].rearrange("p g n -> p (g n)"),
+            in_=w_qk_grouped[:].rearrange("p g e n t -> p (g e n t)"),
+        )
+        w_v_codes = const.tile([P, PASSES, V], U32, name="w_v_codes", align_bytes=64)
+        w_v_scales = const.tile([P, PASSES, V], U8, name="w_v_scales", align_bytes=64)
+        nc.vector.quantize_mx(
+            out=w_v_codes[:].rearrange("p g n -> p (g n)").bitcast(FP8X4),
+            scales=w_v_scales[:].rearrange("p g n -> p (g n)"),
+            in_=w_v_grouped[:].rearrange("p g n t -> p (g n t)"),
         )
 
         def transpose_round(r):
-            grouped = mx_pool.tile([P, ROUND, PASSES, P, PACK], BF16, name="grouped", align_bytes=64)
+            grouped = mx_pool.tile([P, PASSES, ROUND, P, PACK], BF16, name="grouped", align_bytes=64)
             grouped_words = grouped[:].bitcast(F32)
             for a in range(ROUND):
                 tile_in_block = (r * ROUND + a) % BLOCK
@@ -154,32 +163,34 @@ def tile_arlowvisionattention_pa_t_kernel(
                 for j in range(WORD_BLOCKS):
                     nc.tensor.transpose(x_t[:, j, :], words[:, j * P : (j + 1) * P], ident_f32[:])
                 nc.scalar.copy(
-                    out=grouped_words[:, a], in_=x_t[:].rearrange("p (g u) r -> p g r u", u=2)
+                    out=grouped_words[:, :, a], in_=x_t[:].rearrange("p (g u) r -> p g r u", u=2)
                 )
             if (r + 1) * ROUND % BLOCK == 0 and r * ROUND // BLOCK + X_BUFS < BLOCKS:
                 load_block(r * ROUND // BLOCK + X_BUFS, 1)
             return grouped
 
         def quantise_round(grouped):
-            codes = mx_pool.tile([P, ROUND, PASSES, P], U32, name="codes", align_bytes=64)
-            scales = mx_pool.tile([P, ROUND, PASSES, P], U8, name="scales", align_bytes=64)
+            codes = mx_pool.tile([P, PASSES, ROUND, P], U32, name="codes", align_bytes=64)
+            scales = mx_pool.tile([P, PASSES, ROUND, P], U8, name="scales", align_bytes=64)
             nc.vector.quantize_mx(
-                out=codes[:].rearrange("p a g r -> p (a g r)").bitcast(FP8X4),
-                scales=scales[:].rearrange("p a g r -> p (a g r)"),
-                in_=grouped[:].rearrange("p a g r t -> p (a g r t)"),
+                out=codes[:].rearrange("p g a r -> p (g a r)").bitcast(FP8X4),
+                scales=scales[:].rearrange("p g a r -> p (g a r)"),
+                in_=grouped[:].rearrange("p g a r t -> p (g a r t)"),
             )
             return codes, scales
 
+        tables = {}
         tables_t = const.tile([P, ROUNDS, P], BF16, name="tables_t")
 
-        def transpose_tables(run):
-            first = run * TABLE_RUN * ROUND
-            mixed = rope_pool.tile([P, TABLE_RUN * ROUND, 2, HEAD_DIM], BF16, name="mixed", bufs=2)
-            nc.vector.tensor_copy(
-                out=mixed[:, :, 0, :], in_=cos_sb[:, first : first + TABLE_RUN * ROUND, :]
-            )
-            nc.vector.tensor_copy(
-                out=mixed[:, :, 1, :], in_=sin_sb[:, first : first + TABLE_RUN * ROUND, :]
+        def prepare_tables(run):
+            tiles = slice(run * TABLE_RUN * ROUND, (run + 1) * TABLE_RUN * ROUND)
+            mixed = table_pool.tile([P, TABLE_RUN * ROUND, 2, HEAD_DIM], BF16, name="mixed")
+            nc.vector.tensor_copy(out=mixed[:, :, 0, :], in_=cos_sb[:, tiles, :])
+            nc.vector.tensor_tensor(
+                out=mixed[:, :, 1, :],
+                in0=sin_sb[:, tiles, :],
+                in1=signs[:].unsqueeze(1).to_broadcast([P, TABLE_RUN * ROUND, HEAD_DIM]),
+                op=MULT,
             )
             mixed_t = psum_t.tile([P, TABLE_RUN, P], BF16, name="mixed_t", tag="t")
             for r in range(TABLE_RUN):
@@ -191,23 +202,33 @@ def tile_arlowvisionattention_pa_t_kernel(
             nc.scalar.copy(
                 out=tables_t[:, run * TABLE_RUN : (run + 1) * TABLE_RUN, :], in_=mixed_t[:]
             )
+            tables[run] = mixed
 
         def project_round(r, codes_and_scales):
             codes, scales = codes_and_scales
-            accs = []
+            qk = psum_qk.tile([P, ROUND, QK], F32, name="qk", tag="qk")
             for a in range(ROUND):
-                acc = psum_acc.tile([P, MOVING], F32, name="acc", tag="acc")
                 for g in range(PASSES):
                     nc.tensor.matmul_mx(
-                        out=acc[:],
-                        lhsT=codes[:, a, g, :].bitcast(FP8X4),
-                        lhsT_scale=scales[:, a, g, :],
-                        rhs=w_codes[:, g, :].bitcast(FP8X4),
-                        rhs_scale=w_scales[:, g, :],
+                        out=qk[:, a, :],
+                        lhsT=codes[:, g, a, :].bitcast(FP8X4),
+                        lhsT_scale=scales[:, g, a, :],
+                        rhs=w_qk_codes[:, g, :].bitcast(FP8X4),
+                        rhs_scale=w_qk_scales[:, g, :],
                         start=(g == 0),
                         stop=(g == PASSES - 1),
                     )
-                accs.append(acc)
+            v_t = psum_v.tile([P, ROUND * P], F32, name="v_t")
+            for g in range(PASSES):
+                nc.tensor.matmul_mx(
+                    out=v_t[:],
+                    lhsT=w_v_codes[:, g, :].bitcast(FP8X4),
+                    lhsT_scale=w_v_scales[:, g, :],
+                    rhs=codes[:, g].rearrange("p a r -> p (a r)").bitcast(FP8X4),
+                    rhs_scale=scales[:, g].rearrange("p a r -> p (a r)"),
+                    start=(g == 0),
+                    stop=(g == PASSES - 1),
+                )
             bias_share = psum_bias.tile([P, ROUND, QK], F32, name="bias_share")
             nc.tensor.matmul(
                 out=bias_share[:].rearrange("p a n -> p (a n)"),
@@ -216,37 +237,40 @@ def tile_arlowvisionattention_pa_t_kernel(
                 start=True,
                 stop=True,
             )
-            return accs, bias_share
+            v_t_sb = rope_pool.tile([P, ROUND * P], F32, name="v_t_sb")
+            nc.scalar.activation(
+                out=v_t_sb[:], in_=v_t[:], func=IDENTITY, bias=bias_v[:, 0:1], scale=1.0
+            )
+            return qk, bias_share, v_t_sb
 
-        def table_of(table_sb, m):
-            pairs = table_sb[:, m, :].rearrange("p (i e) -> p i e", e=2)
-            return pairs.unsqueeze(1).to_broadcast([P, QK_HEADS, PAIRS, 2])
-
-        def copy_v_round(r, accs, out_blk):
+        def return_v_round(r, v_t_sb, out_blk):
+            v_back = psum_v.tile([P, ROUND, P], F32, name="v_back")
             for a in range(ROUND):
-                nc.scalar.copy(
-                    out=out_blk[:, 2, (r * ROUND + a) % BLOCK, :],
-                    in_=accs[a][:, 3 * GROUP : 4 * GROUP],
-                )
+                nc.tensor.transpose(v_back[:, a, :], v_t_sb[:, a * P : (a + 1) * P], ident_f32[:])
+            first = r * ROUND % BLOCK
+            nc.scalar.copy(out=out_blk[:, 2, first : first + ROUND, :], in_=v_back[:])
 
-        def multiply_round(r, accs):
-            by_cos = rope_pool.tile([P, ROUND, QK_HEADS, PAIRS, 2], F32, name="by_cos")
-            by_sin = rope_pool.tile([P, ROUND, QK_HEADS, PAIRS, 2], F32, name="by_sin")
-            for a in range(ROUND):
-                m = r * ROUND + a
-                groups = accs[a][:, 0 : 3 * GROUP].rearrange("p (w h i) -> p w h i", w=3, i=PAIRS)
-                nc.vector.tensor_tensor(
-                    out=by_cos[:, a],
-                    in0=groups[:, 1:3].rearrange("p e h i -> p h i e"),
-                    in1=table_of(cos_sb, m),
-                    op=MULT,
-                )
-                nc.vector.tensor_tensor(
-                    out=by_sin[:, a],
-                    in0=groups[:, 0:2].rearrange("p e h i -> p h i e"),
-                    in1=table_of(sin_sb, m),
-                    op=MULT,
-                )
+        def multiply_round(r, qk):
+            shape = [P, ROUND, QK_HEADS, PAIRS, 2]
+            first = r % TABLE_RUN * ROUND
+            table = tables[r // TABLE_RUN][:, first : first + ROUND, :, :].rearrange(
+                "p a s (i e) -> p s a i e", e=2
+            )
+            halves = qk[:].rearrange("p a (e h i) -> p a e h i", e=2, i=PAIRS)
+            by_cos = rope_pool.tile(shape, F32, name="by_cos")
+            nc.vector.tensor_tensor(
+                out=by_cos[:],
+                in0=halves.rearrange("p a e h i -> p a h i e"),
+                in1=table[:, 0].unsqueeze(2).to_broadcast(shape),
+                op=MULT,
+            )
+            by_sin = rope_pool.tile(shape, F32, name="by_sin")
+            nc.vector.tensor_tensor(
+                out=by_sin[:],
+                in0=halves[:, :, ::-1].rearrange("p a e h i -> p a h i e"),
+                in1=table[:, 1].unsqueeze(2).to_broadcast(shape),
+                op=MULT,
+            )
             return by_cos, by_sin
 
         def add_bias_share(by_cos, bias_share):
@@ -268,40 +292,32 @@ def tile_arlowvisionattention_pa_t_kernel(
                 op=ADD,
             )
 
-        def finish_v_round(r, out_blk):
-            first = r * ROUND % BLOCK
-            v_rows = out_blk[:, 2, first : first + ROUND, :]
-            bias_v = bias_all[:, QK : QK + GROUP].unsqueeze(1).to_broadcast([P, ROUND, GROUP])
-            nc.gpsimd.tensor_tensor(out=v_rows, in0=v_rows, in1=bias_v, op=ADD)
-
-        quantised, products, out_blks = {}, {}, {}
+        quantised, products = {}, {}
+        out_blk = None
         for r in range(-2, ROUNDS):
             grouped = None
             if r + 2 < ROUNDS:
                 grouped = transpose_round(r + 2)
                 if (r + 2) % TABLE_RUN == 0:
-                    transpose_tables((r + 2) // TABLE_RUN)
+                    prepare_tables((r + 2) // TABLE_RUN)
+            if r >= 0:
+                qk, bias_share, v_t_sb = products[r]
+                if r * ROUND % BLOCK == 0:
+                    out_blk = out_pool.tile([P, 3, BLOCK, V], F32, name="out_blk")
+                return_v_round(r, v_t_sb, out_blk)
             if 0 <= r + 1 < ROUNDS:
                 products[r + 1] = project_round(r + 1, quantised[r + 1])
-                if (r + 1) * ROUND % BLOCK == 0:
-                    out_blks[(r + 1) * ROUND // BLOCK] = out_pool.tile(
-                        [P, 3, BLOCK, GROUP], F32, name="out_blk"
-                    )
-                copy_v_round(r + 1, products[r + 1][0], out_blks[(r + 1) * ROUND // BLOCK])
             if r >= 0:
-                accs, bias_share = products[r]
-                by_cos, by_sin = multiply_round(r, accs)
+                by_cos, by_sin = multiply_round(r, qk)
                 summed = add_bias_share(by_cos, bias_share)
             if r + 2 < ROUNDS:
                 quantised[r + 2] = quantise_round(grouped)
             if r >= 0:
-                finish_qk_round(r, summed, by_sin, out_blks[r * ROUND // BLOCK])
-            if 0 <= r + 1 < ROUNDS:
-                finish_v_round(r + 1, out_blks[(r + 1) * ROUND // BLOCK])
-            if r >= 0 and (r + 1) * ROUND % BLOCK == 0:
-                b = r * ROUND // BLOCK
-                for j in range(3):
-                    nc.sync.dma_start(
-                        out=out_views[j][:, b * BLOCK : (b + 1) * BLOCK, :],
-                        in_=out_blks[b][:, j, :, :],
-                    )
+                finish_qk_round(r, summed, by_sin, out_blk)
+                if (r + 1) * ROUND % BLOCK == 0:
+                    b = r * ROUND // BLOCK
+                    for j in range(3):
+                        nc.sync.dma_start(
+                            out=out_views[j][:, b * BLOCK : (b + 1) * BLOCK, :],
+                            in_=out_blk[:, j, :, :],
+                        )

@@ -20,7 +20,9 @@ HEAD_DIM = 32
 PAIRS = HEAD_DIM // 2
 QK_HEADS = 8
 QK = QK_HEADS * HEAD_DIM
+HALF = QK // 2
 V = 4 * HEAD_DIM
+BANK = 512
 PASSES = HIDDEN // (P * PACK)
 WORD_BLOCKS = HIDDEN // (2 * P)
 TILES = TOKENS // P
@@ -29,7 +31,7 @@ ROUNDS = TILES // ROUND
 BLOCK = 4
 BLOCKS = TILES // BLOCK
 X_BUFS = 3
-TABLE_RUN = 8
+TABLE_PARTS = {0: 16, 16: TILES}
 
 FLOPS = 2 * TOKENS * HIDDEN * (QK + V)
 
@@ -46,12 +48,11 @@ def tile_arlowvisionattention_pa_t_kernel(
         x_pool = ctx.enter_context(tc.tile_pool(name="x", bufs=X_BUFS))
         mx_pool = ctx.enter_context(tc.tile_pool(name="mx", bufs=3))
         rope_pool = ctx.enter_context(tc.tile_pool(name="rope", bufs=3))
-        table_pool = ctx.enter_context(tc.tile_pool(name="table", bufs=2))
         out_pool = ctx.enter_context(tc.tile_pool(name="out", bufs=3))
-        psum_t = ctx.enter_context(tc.psum_pool(name="psum_t", bufs=2))
+        psum_x = ctx.enter_context(tc.psum_pool(name="psum_x", bufs=2))
+        psum_qk_t = ctx.enter_context(tc.psum_pool(name="psum_qk_t", bufs=2))
         psum_qk = ctx.enter_context(tc.psum_pool(name="psum_qk", bufs=2))
-        psum_bias = ctx.enter_context(tc.psum_pool(name="psum_bias", bufs=2))
-        psum_v = ctx.enter_context(tc.psum_pool(name="psum_v", bufs=1))
+        psum_v = ctx.enter_context(tc.psum_pool(name="psum_v", bufs=2))
         ctx.enter_context(tc.manual_schedule())
 
         x_blocks = {}
@@ -75,18 +76,18 @@ def tile_arlowvisionattention_pa_t_kernel(
                     in_=table.rearrange("(p m) d -> p m d", m=TILES)[:, first:last, :],
                 )
 
-        bias_row = const.tile([P, QK + V], BF16, name="bias_row")
+        bias_row = const.tile([P, BANK], BF16, name="bias_row")
         nc.vector.memset(bias_row[:], 0.0)
-        nc.sync.dma_start(out=bias_row[0:1, :], in_=b_qkv.rearrange("(o n) -> o n", o=1))
+        nc.sync.dma_start(out=bias_row[0:1, 0 : QK + V], in_=b_qkv.rearrange("(o n) -> o n", o=1))
         w_raw = const.tile([P, PASSES * 2, 2, QK + V], BF16, name="w_raw")
         nc.sync.dma_start(
             out=w_raw[:], in_=w_qkv.rearrange("(gu p e) c -> p gu e c", gu=PASSES * 2, e=2)
         )
         load_block(0, BLOCK // ROUND)
-        load_tables(0, TABLE_RUN * ROUND)
+        load_tables(0, TABLE_PARTS[0])
         for b in range(1, X_BUFS):
             load_block(b, 1)
-        load_tables(TABLE_RUN * ROUND, TILES)
+        load_tables(TABLE_PARTS[0], TILES)
 
         ident_f32 = const.tile([P, P], F32, name="ident_f32")
         make_identity(nc, ident_f32[:])
@@ -95,54 +96,34 @@ def tile_arlowvisionattention_pa_t_kernel(
 
         ones = const.tile([P, P], BF16, name="ones")
         nc.vector.memset(ones[:], 1.0)
-        bias_spread = psum_qk.tile([P, QK], F32, name="bias_spread", tag="qk")
-        nc.tensor.matmul(
-            out=bias_spread[:], lhsT=ones[:], rhs=bias_row[:, 0:QK], start=True, stop=True
-        )
-        bias_qk = const.tile([P, QK], BF16, name="bias_qk")
-        nc.scalar.copy(out=bias_qk[:], in_=bias_spread[:])
-        bias_row_t = psum_t.tile([P, P], BF16, name="bias_row_t", tag="t")
-        nc.tensor.transpose(bias_row_t[:], bias_row[:, QK : QK + V], ident_bf16[:])
-        bias_v = const.tile([P, 1], F32, name="bias_v")
-        nc.scalar.copy(out=bias_v[:], in_=bias_row_t[:, 0:1])
-
-        bias_swap = const.tile([P, QK], BF16, name="bias_swap")
+        bias_spread = psum_qk.tile([P, BANK], F32, name="bias_spread", tag="qk")
+        nc.tensor.matmul(out=bias_spread[:], lhsT=ones[:], rhs=bias_row[:], start=True, stop=True)
+        bias_v = const.tile([P, V], BF16, name="bias_v")
+        nc.scalar.copy(out=bias_v[:], in_=bias_spread[:, QK : QK + V])
+        bias_sorted = const.tile([P, 2, HALF], BF16, name="bias_sorted")
         nc.vector.tensor_copy(
-            out=bias_swap[:].rearrange("p (n e) -> p n e", e=2),
-            in_=bias_qk[:].rearrange("p (n e) -> p n e", e=2)[:, :, ::-1],
+            out=bias_sorted[:], in_=bias_row[:, 0:QK].rearrange("p (n e) -> p e n", e=2)
         )
-        select = ident_bf16[:].rearrange("p (a s d) -> p a s d", a=ROUND, s=2)
-        full = [P, ROUND, QK_HEADS, HEAD_DIM]
-        bias_rhs = const.tile([P, ROUND, QK], BF16, name="bias_rhs")
-        sin_rows = const.tile([P, ROUND, QK], BF16, name="sin_rows")
-        for rows, s, bias in ((bias_rhs, 0, bias_qk), (sin_rows, 1, bias_swap)):
-            nc.vector.tensor_tensor(
-                out=rows[:].rearrange("p a (h d) -> p a h d", d=HEAD_DIM),
-                in0=select[:, :, s, :].unsqueeze(2).to_broadcast(full),
-                in1=bias[:].rearrange("p (h d) -> p h d", d=HEAD_DIM).unsqueeze(1).to_broadcast(full),
-                op=MULT,
-            )
-        nc.vector.tensor_tensor(out=bias_rhs[:], in0=bias_rhs[:], in1=sin_rows[:], op=ADD)
-        signs = const.tile([P, HEAD_DIM], BF16, name="signs")
-        nc.vector.memset(signs[:], 1.0)
-        nc.vector.memset(signs[:].rearrange("p (i e) -> p i e", e=2)[:, :, 0], -1.0)
+        bias_sorted_t = psum_x.tile([P, 2, P], BF16, name="bias_sorted_t", tag="x_t")
+        for e in range(2):
+            nc.tensor.transpose(bias_sorted_t[:, e, :], bias_sorted[:, e, :], ident_bf16[:])
+        bias_qk = const.tile([P, 2], F32, name="bias_qk")
+        nc.scalar.copy(out=bias_qk[:], in_=bias_sorted_t[:, :, 0])
 
         w_rows = w_raw[:].rearrange("p (g u) e c -> p g (u e) c", u=2)
         w_halves = w_rows[:, :, :, 0:QK].rearrange("p g t (n e) -> p e g n t", e=2)
-        w_qk_grouped = const.tile(
-            [P, PASSES, 2, QK // 2, PACK], BF16, name="w_qk_grouped", align_bytes=64
-        )
+        w_qk_grouped = const.tile([P, PASSES, 2, HALF, PACK], BF16, name="w_qk_grouped", align_bytes=64)
         nc.vector.tensor_copy(out=w_qk_grouped[:, :, 0], in_=w_halves[:, 0])
         nc.scalar.copy(out=w_qk_grouped[:, :, 1], in_=w_halves[:, 1])
         w_v_grouped = const.tile([P, PASSES, V, PACK], BF16, name="w_v_grouped", align_bytes=64)
         nc.vector.tensor_copy(
             out=w_v_grouped[:], in_=w_rows[:, :, :, QK : QK + V].rearrange("p g t n -> p g n t")
         )
-        w_qk_codes = const.tile([P, PASSES, QK], U32, name="w_qk_codes", align_bytes=64)
-        w_qk_scales = const.tile([P, PASSES, QK], U8, name="w_qk_scales", align_bytes=64)
+        w_qk_codes = const.tile([P, PASSES, 2, HALF], U32, name="w_qk_codes", align_bytes=64)
+        w_qk_scales = const.tile([P, PASSES, 2, HALF], U8, name="w_qk_scales", align_bytes=64)
         nc.vector.quantize_mx(
-            out=w_qk_codes[:].rearrange("p g n -> p (g n)").bitcast(FP8X4),
-            scales=w_qk_scales[:].rearrange("p g n -> p (g n)"),
+            out=w_qk_codes[:].rearrange("p g e n -> p (g e n)").bitcast(FP8X4),
+            scales=w_qk_scales[:].rearrange("p g e n -> p (g e n)"),
             in_=w_qk_grouped[:].rearrange("p g e n t -> p (g e n t)"),
         )
         w_v_codes = const.tile([P, PASSES, V], U32, name="w_v_codes", align_bytes=64)
@@ -153,13 +134,25 @@ def tile_arlowvisionattention_pa_t_kernel(
             in_=w_v_grouped[:].rearrange("p g n t -> p (g n t)"),
         )
 
+        signs = const.tile([P, HEAD_DIM], BF16, name="signs")
+        nc.vector.memset(signs[:], 1.0)
+        nc.vector.memset(signs[:].rearrange("p (i e) -> p i e", e=2)[:, :, 0], -1.0)
+
+        def sign_sin(first, last):
+            nc.vector.tensor_tensor(
+                out=sin_sb[:, first:last, :],
+                in0=sin_sb[:, first:last, :],
+                in1=signs[:].unsqueeze(1).to_broadcast([P, last - first, HEAD_DIM]),
+                op=MULT,
+            )
+
         def transpose_round(r):
             grouped = mx_pool.tile([P, PASSES, ROUND, P, PACK], BF16, name="grouped", align_bytes=64)
             grouped_words = grouped[:].bitcast(F32)
             for a in range(ROUND):
                 tile_in_block = (r * ROUND + a) % BLOCK
                 words = x_blocks[r * ROUND // BLOCK][:, tile_in_block, :].bitcast(F32)
-                x_t = psum_t.tile([P, WORD_BLOCKS, P], F32, name="x_t", tag="t")
+                x_t = psum_x.tile([P, WORD_BLOCKS, P], F32, name="x_t", tag="x_t")
                 for j in range(WORD_BLOCKS):
                     nc.tensor.transpose(x_t[:, j, :], words[:, j * P : (j + 1) * P], ident_f32[:])
                 nc.scalar.copy(
@@ -179,145 +172,117 @@ def tile_arlowvisionattention_pa_t_kernel(
             )
             return codes, scales
 
-        tables = {}
-        tables_t = const.tile([P, ROUNDS, P], BF16, name="tables_t")
-
-        def prepare_tables(run):
-            tiles = slice(run * TABLE_RUN * ROUND, (run + 1) * TABLE_RUN * ROUND)
-            mixed = table_pool.tile([P, TABLE_RUN * ROUND, 2, HEAD_DIM], BF16, name="mixed")
-            nc.vector.tensor_copy(out=mixed[:, :, 0, :], in_=cos_sb[:, tiles, :])
-            nc.vector.tensor_tensor(
-                out=mixed[:, :, 1, :],
-                in0=sin_sb[:, tiles, :],
-                in1=signs[:].unsqueeze(1).to_broadcast([P, TABLE_RUN * ROUND, HEAD_DIM]),
-                op=MULT,
-            )
-            mixed_t = psum_t.tile([P, TABLE_RUN, P], BF16, name="mixed_t", tag="t")
-            for r in range(TABLE_RUN):
-                nc.tensor.transpose(
-                    mixed_t[:, r, :],
-                    mixed[:, r * ROUND : (r + 1) * ROUND, :, :].rearrange("p a s d -> p (a s d)"),
-                    ident_bf16[:],
-                )
-            nc.scalar.copy(
-                out=tables_t[:, run * TABLE_RUN : (run + 1) * TABLE_RUN, :], in_=mixed_t[:]
-            )
-            tables[run] = mixed
-
-        def project_round(r, codes_and_scales):
+        def project_round(codes_and_scales):
             codes, scales = codes_and_scales
-            qk = psum_qk.tile([P, ROUND, QK], F32, name="qk", tag="qk")
-            for a in range(ROUND):
+            qk_t = psum_qk_t.tile([P, 2, ROUND * P], F32, name="qk_t")
+            for e in range(2):
                 for g in range(PASSES):
                     nc.tensor.matmul_mx(
-                        out=qk[:, a, :],
-                        lhsT=codes[:, g, a, :].bitcast(FP8X4),
-                        lhsT_scale=scales[:, g, a, :],
-                        rhs=w_qk_codes[:, g, :].bitcast(FP8X4),
-                        rhs_scale=w_qk_scales[:, g, :],
+                        out=qk_t[:, e, :],
+                        lhsT=w_qk_codes[:, g, e, :].bitcast(FP8X4),
+                        lhsT_scale=w_qk_scales[:, g, e, :],
+                        rhs=codes[:, g].rearrange("p a r -> p (a r)").bitcast(FP8X4),
+                        rhs_scale=scales[:, g].rearrange("p a r -> p (a r)"),
                         start=(g == 0),
                         stop=(g == PASSES - 1),
                     )
-            v_t = psum_v.tile([P, ROUND * P], F32, name="v_t")
-            for g in range(PASSES):
-                nc.tensor.matmul_mx(
-                    out=v_t[:],
-                    lhsT=w_v_codes[:, g, :].bitcast(FP8X4),
-                    lhsT_scale=w_v_scales[:, g, :],
-                    rhs=codes[:, g].rearrange("p a r -> p (a r)").bitcast(FP8X4),
-                    rhs_scale=scales[:, g].rearrange("p a r -> p (a r)"),
-                    start=(g == 0),
-                    stop=(g == PASSES - 1),
-                )
-            bias_share = psum_bias.tile([P, ROUND, QK], F32, name="bias_share")
-            nc.tensor.matmul(
-                out=bias_share[:].rearrange("p a n -> p (a n)"),
-                lhsT=tables_t[:, r, :],
-                rhs=bias_rhs[:].rearrange("p a n -> p (a n)"),
-                start=True,
-                stop=True,
-            )
-            v_t_sb = rope_pool.tile([P, ROUND * P], F32, name="v_t_sb")
-            nc.scalar.activation(
-                out=v_t_sb[:], in_=v_t[:], func=IDENTITY, bias=bias_v[:, 0:1], scale=1.0
-            )
-            return qk, bias_share, v_t_sb
-
-        def return_v_round(r, v_t_sb, out_blk):
-            v_back = psum_v.tile([P, ROUND, P], F32, name="v_back")
+            v = psum_v.tile([P, ROUND, V], F32, name="v")
             for a in range(ROUND):
-                nc.tensor.transpose(v_back[:, a, :], v_t_sb[:, a * P : (a + 1) * P], ident_f32[:])
-            first = r * ROUND % BLOCK
-            nc.scalar.copy(out=out_blk[:, 2, first : first + ROUND, :], in_=v_back[:])
+                for g in range(PASSES):
+                    nc.tensor.matmul_mx(
+                        out=v[:, a, :],
+                        lhsT=codes[:, g, a, :].bitcast(FP8X4),
+                        lhsT_scale=scales[:, g, a, :],
+                        rhs=w_v_codes[:, g, :].bitcast(FP8X4),
+                        rhs_scale=w_v_scales[:, g, :],
+                        start=(g == 0),
+                        stop=(g == PASSES - 1),
+                    )
+            qk_t_sb = rope_pool.tile([P, 2, ROUND * P], F32, name="qk_t_sb")
+            for e in range(2):
+                nc.scalar.activation(
+                    out=qk_t_sb[:, e, :],
+                    in_=qk_t[:, e, :],
+                    func=IDENTITY,
+                    bias=bias_qk[:, e : e + 1],
+                    scale=1.0,
+                )
+            return qk_t_sb, v
+
+        def turn_back_round(qk_t_sb):
+            qk = psum_qk.tile([P, ROUND, 2, HALF], F32, name="qk", tag="qk")
+            for a in range(ROUND):
+                for e in range(2):
+                    nc.tensor.transpose(
+                        qk[:, a, e, :], qk_t_sb[:, e, a * P : (a + 1) * P], ident_f32[:]
+                    )
+            return qk
 
         def multiply_round(r, qk):
             shape = [P, ROUND, QK_HEADS, PAIRS, 2]
-            first = r % TABLE_RUN * ROUND
-            table = tables[r // TABLE_RUN][:, first : first + ROUND, :, :].rearrange(
-                "p a s (i e) -> p s a i e", e=2
-            )
-            halves = qk[:].rearrange("p a (e h i) -> p a e h i", e=2, i=PAIRS)
+            tiles = slice(r * ROUND, (r + 1) * ROUND)
+            halves = qk[:].rearrange("p a e (h i) -> p a e h i", i=PAIRS)
             by_cos = rope_pool.tile(shape, F32, name="by_cos")
             nc.vector.tensor_tensor(
                 out=by_cos[:],
                 in0=halves.rearrange("p a e h i -> p a h i e"),
-                in1=table[:, 0].unsqueeze(2).to_broadcast(shape),
+                in1=cos_sb[:, tiles, :].rearrange("p a (i e) -> p a i e", e=2).unsqueeze(2).to_broadcast(shape),
                 op=MULT,
             )
             by_sin = rope_pool.tile(shape, F32, name="by_sin")
             nc.vector.tensor_tensor(
                 out=by_sin[:],
                 in0=halves[:, :, ::-1].rearrange("p a e h i -> p a h i e"),
-                in1=table[:, 1].unsqueeze(2).to_broadcast(shape),
+                in1=sin_sb[:, tiles, :].rearrange("p a (i e) -> p a i e", e=2).unsqueeze(2).to_broadcast(shape),
                 op=MULT,
             )
             return by_cos, by_sin
 
-        def add_bias_share(by_cos, bias_share):
-            summed = rope_pool.tile([P, ROUND, QK], F32, name="summed")
-            nc.vector.tensor_tensor(
-                out=summed[:],
-                in0=by_cos[:].rearrange("p a h i e -> p a (h i e)"),
-                in1=bias_share[:],
-                op=ADD,
-            )
-            return summed
-
-        def finish_qk_round(r, summed, by_sin, out_blk):
+        def finish_qk_round(r, by_cos, by_sin, out_blk):
             first = r * ROUND % BLOCK
             nc.gpsimd.tensor_tensor(
                 out=out_blk[:, 0:2, first : first + ROUND, :],
-                in0=summed[:].rearrange("p a (j n) -> p j a n", j=2),
+                in0=by_cos[:].rearrange("p a (j h) i e -> p j a (h i e)", j=2),
                 in1=by_sin[:].rearrange("p a (j h) i e -> p j a (h i e)", j=2),
                 op=ADD,
             )
 
-        quantised, products = {}, {}
-        out_blk = None
-        for r in range(-2, ROUNDS):
+        def finish_v_round(r, v, out_blk):
+            first = r * ROUND % BLOCK
+            nc.vector.tensor_tensor(
+                out=out_blk[:, 2, first : first + ROUND, :],
+                in0=v[:],
+                in1=bias_v[:].unsqueeze(1).to_broadcast([P, ROUND, V]),
+                op=ADD,
+            )
+
+        quantised, projected, turned_back, out_blks = {}, {}, {}, {}
+        for r in range(-3, ROUNDS):
             grouped = None
-            if r + 2 < ROUNDS:
-                grouped = transpose_round(r + 2)
-                if (r + 2) % TABLE_RUN == 0:
-                    prepare_tables((r + 2) // TABLE_RUN)
-            if r >= 0:
-                qk, bias_share, v_t_sb = products[r]
-                if r * ROUND % BLOCK == 0:
-                    out_blk = out_pool.tile([P, 3, BLOCK, V], F32, name="out_blk")
-                return_v_round(r, v_t_sb, out_blk)
+            if r + 3 < ROUNDS:
+                grouped = transpose_round(r + 3)
             if 0 <= r + 1 < ROUNDS:
-                products[r + 1] = project_round(r + 1, quantised[r + 1])
+                turned_back[r + 1] = turn_back_round(projected[r + 1][0])
+            if 0 <= r + 2 < ROUNDS:
+                projected[r + 2] = project_round(quantised[r + 2])
+            if (r + 1) * ROUND in TABLE_PARTS:
+                sign_sin((r + 1) * ROUND, TABLE_PARTS[(r + 1) * ROUND])
             if r >= 0:
-                by_cos, by_sin = multiply_round(r, qk)
-                summed = add_bias_share(by_cos, bias_share)
-            if r + 2 < ROUNDS:
-                quantised[r + 2] = quantise_round(grouped)
-            if r >= 0:
-                finish_qk_round(r, summed, by_sin, out_blk)
+                by_cos, by_sin = multiply_round(r, turned_back[r])
+            if r + 3 < ROUNDS:
+                quantised[r + 3] = quantise_round(grouped)
+            if 0 <= r + 1 < ROUNDS:
                 if (r + 1) * ROUND % BLOCK == 0:
-                    b = r * ROUND // BLOCK
+                    out_blks[(r + 1) * ROUND // BLOCK] = out_pool.tile(
+                        [P, 3, BLOCK, V], F32, name="out_blk"
+                    )
+                finish_v_round(r + 1, projected[r + 1][1], out_blks[(r + 1) * ROUND // BLOCK])
+            if r >= 0:
+                b = r * ROUND // BLOCK
+                finish_qk_round(r, by_cos, by_sin, out_blks[b])
+                if (r + 1) * ROUND % BLOCK == 0:
                     for j in range(3):
                         nc.sync.dma_start(
                             out=out_views[j][:, b * BLOCK : (b + 1) * BLOCK, :],
-                            in_=out_blk[:, j, :, :],
+                            in_=out_blks[b][:, j, :, :],
                         )

@@ -57,14 +57,14 @@ def tile_arlowvisionattention_pa_t_kernel(
 
         x_blocks = {}
 
-        def load_block(b, pieces):
-            x_blocks[b] = x_pool.tile([P, BLOCK, HIDDEN], BF16, name="x_blk")
-            step = BLOCK // pieces
-            for first in range(0, BLOCK, step):
-                nc.sync.dma_start(
-                    out=x_blocks[b][:, first : first + step, :],
-                    in_=x_view[:, b * BLOCK + first : b * BLOCK + first + step, :],
-                )
+        def load_tiles(first, count):
+            b = first // BLOCK
+            if first % BLOCK == 0:
+                x_blocks[b] = x_pool.tile([P, BLOCK, HIDDEN], BF16, name="x_blk")
+            nc.sync.dma_start(
+                out=x_blocks[b][:, first % BLOCK : first % BLOCK + count, :],
+                in_=x_view[:, first : first + count, :],
+            )
 
         cos_sb = const.tile([P, TILES, HEAD_DIM], BF16, name="cos_sb")
         sin_sb = const.tile([P, TILES, HEAD_DIM], BF16, name="sin_sb")
@@ -79,14 +79,15 @@ def tile_arlowvisionattention_pa_t_kernel(
         bias_row = const.tile([P, BANK], BF16, name="bias_row")
         nc.vector.memset(bias_row[:], 0.0)
         nc.sync.dma_start(out=bias_row[0:1, 0 : QK + V], in_=b_qkv.rearrange("(o n) -> o n", o=1))
+        load_tiles(0, ROUND)
         w_raw = const.tile([P, PASSES * 2, 2, QK + V], BF16, name="w_raw")
         nc.sync.dma_start(
             out=w_raw[:], in_=w_qkv.rearrange("(gu p e) c -> p gu e c", gu=PASSES * 2, e=2)
         )
-        load_block(0, BLOCK // ROUND)
+        load_tiles(ROUND, ROUND)
         load_tables(0, TABLE_PARTS[0])
-        for b in range(1, X_BUFS):
-            load_block(b, 1)
+        for first in range(BLOCK, X_BUFS * BLOCK, ROUND):
+            load_tiles(first, ROUND)
         load_tables(TABLE_PARTS[0], TILES)
 
         ident_f32 = const.tile([P, P], F32, name="ident_f32")
@@ -110,41 +111,9 @@ def tile_arlowvisionattention_pa_t_kernel(
         bias_qk = const.tile([P, 2], F32, name="bias_qk")
         nc.scalar.copy(out=bias_qk[:], in_=bias_sorted_t[:, :, 0])
 
-        w_rows = w_raw[:].rearrange("p (g u) e c -> p g (u e) c", u=2)
-        w_halves = w_rows[:, :, :, 0:QK].rearrange("p g t (n e) -> p e g n t", e=2)
-        w_qk_grouped = const.tile([P, PASSES, 2, HALF, PACK], BF16, name="w_qk_grouped", align_bytes=64)
-        nc.vector.tensor_copy(out=w_qk_grouped[:, :, 0], in_=w_halves[:, 0])
-        nc.scalar.copy(out=w_qk_grouped[:, :, 1], in_=w_halves[:, 1])
-        w_v_grouped = const.tile([P, PASSES, V, PACK], BF16, name="w_v_grouped", align_bytes=64)
-        nc.vector.tensor_copy(
-            out=w_v_grouped[:], in_=w_rows[:, :, :, QK : QK + V].rearrange("p g t n -> p g n t")
-        )
-        w_qk_codes = const.tile([P, PASSES, 2, HALF], U32, name="w_qk_codes", align_bytes=64)
-        w_qk_scales = const.tile([P, PASSES, 2, HALF], U8, name="w_qk_scales", align_bytes=64)
-        nc.vector.quantize_mx(
-            out=w_qk_codes[:].rearrange("p g e n -> p (g e n)").bitcast(FP8X4),
-            scales=w_qk_scales[:].rearrange("p g e n -> p (g e n)"),
-            in_=w_qk_grouped[:].rearrange("p g e n t -> p (g e n t)"),
-        )
-        w_v_codes = const.tile([P, PASSES, V], U32, name="w_v_codes", align_bytes=64)
-        w_v_scales = const.tile([P, PASSES, V], U8, name="w_v_scales", align_bytes=64)
-        nc.vector.quantize_mx(
-            out=w_v_codes[:].rearrange("p g n -> p (g n)").bitcast(FP8X4),
-            scales=w_v_scales[:].rearrange("p g n -> p (g n)"),
-            in_=w_v_grouped[:].rearrange("p g n t -> p (g n t)"),
-        )
-
-        signs = const.tile([P, HEAD_DIM], BF16, name="signs")
-        nc.vector.memset(signs[:], 1.0)
-        nc.vector.memset(signs[:].rearrange("p (i e) -> p i e", e=2)[:, :, 0], -1.0)
-
         def sign_sin(first, last):
-            nc.vector.tensor_tensor(
-                out=sin_sb[:, first:last, :],
-                in0=sin_sb[:, first:last, :],
-                in1=signs[:].unsqueeze(1).to_broadcast([P, last - first, HEAD_DIM]),
-                op=MULT,
-            )
+            even = sin_sb[:, first:last, :].rearrange("p m (i e) -> p m i e", e=2)[:, :, :, 0]
+            nc.scalar.mul(out=even, in_=even, mul=-1.0)
 
         def transpose_round(r):
             grouped = mx_pool.tile([P, PASSES, ROUND, P, PACK], BF16, name="grouped", align_bytes=64)
@@ -159,7 +128,7 @@ def tile_arlowvisionattention_pa_t_kernel(
                     out=grouped_words[:, :, a], in_=x_t[:].rearrange("p (g u) r -> p g r u", u=2)
                 )
             if (r + 1) * ROUND % BLOCK == 0 and r * ROUND // BLOCK + X_BUFS < BLOCKS:
-                load_block(r * ROUND // BLOCK + X_BUFS, 1)
+                load_tiles((r * ROUND // BLOCK + X_BUFS) * BLOCK, BLOCK)
             return grouped
 
         def quantise_round(grouped):
@@ -256,8 +225,41 @@ def tile_arlowvisionattention_pa_t_kernel(
                 op=ADD,
             )
 
-        quantised, projected, turned_back, out_blks = {}, {}, {}, {}
-        for r in range(-3, ROUNDS):
+        def store_tiles(out_blk, first, count):
+            for j in range(3):
+                nc.sync.dma_start(
+                    out=out_views[j][:, first : first + count, :],
+                    in_=out_blk[:, j, first % BLOCK : first % BLOCK + count, :],
+                )
+
+        quantised = {0: quantise_round(transpose_round(0))}
+
+        w_rows = w_raw[:].rearrange("p (g u) e c -> p g (u e) c", u=2)
+        w_halves = w_rows[:, :, :, 0:QK].rearrange("p g t (n e) -> p e g n t", e=2)
+        w_qk_grouped = const.tile([P, PASSES, 2, HALF, PACK], BF16, name="w_qk_grouped", align_bytes=64)
+        nc.vector.tensor_copy(out=w_qk_grouped[:, :, 0], in_=w_halves[:, 0])
+        nc.scalar.copy(out=w_qk_grouped[:, :, 1], in_=w_halves[:, 1])
+        w_qk_codes = const.tile([P, PASSES, 2, HALF], U32, name="w_qk_codes", align_bytes=64)
+        w_qk_scales = const.tile([P, PASSES, 2, HALF], U8, name="w_qk_scales", align_bytes=64)
+        nc.vector.quantize_mx(
+            out=w_qk_codes[:].rearrange("p g e n -> p (g e n)").bitcast(FP8X4),
+            scales=w_qk_scales[:].rearrange("p g e n -> p (g e n)"),
+            in_=w_qk_grouped[:].rearrange("p g e n t -> p (g e n t)"),
+        )
+        w_v_grouped = const.tile([P, PASSES, V, PACK], BF16, name="w_v_grouped", align_bytes=64)
+        nc.vector.tensor_copy(
+            out=w_v_grouped[:], in_=w_rows[:, :, :, QK : QK + V].rearrange("p g t n -> p g n t")
+        )
+        w_v_codes = const.tile([P, PASSES, V], U32, name="w_v_codes", align_bytes=64)
+        w_v_scales = const.tile([P, PASSES, V], U8, name="w_v_scales", align_bytes=64)
+        nc.vector.quantize_mx(
+            out=w_v_codes[:].rearrange("p g n -> p (g n)").bitcast(FP8X4),
+            scales=w_v_scales[:].rearrange("p g n -> p (g n)"),
+            in_=w_v_grouped[:].rearrange("p g n t -> p (g n t)"),
+        )
+
+        projected, turned_back, out_blks = {}, {}, {}
+        for r in range(-2, ROUNDS):
             grouped = None
             if r + 3 < ROUNDS:
                 grouped = transpose_round(r + 3)
@@ -280,9 +282,7 @@ def tile_arlowvisionattention_pa_t_kernel(
             if r >= 0:
                 b = r * ROUND // BLOCK
                 finish_qk_round(r, by_cos, by_sin, out_blks[b])
-                if (r + 1) * ROUND % BLOCK == 0:
-                    for j in range(3):
-                        nc.sync.dma_start(
-                            out=out_views[j][:, b * BLOCK : (b + 1) * BLOCK, :],
-                            in_=out_blks[b][:, j, :, :],
-                        )
+                if b == BLOCKS - 1:
+                    store_tiles(out_blks[b], r * ROUND, ROUND)
+                elif (r + 1) * ROUND % BLOCK == 0:
+                    store_tiles(out_blks[b], b * BLOCK, BLOCK)

@@ -111,9 +111,17 @@ def tile_arlowvisionattention_pa_t_kernel(
         bias_qk = const.tile([P, 2], F32, name="bias_qk")
         nc.scalar.copy(out=bias_qk[:], in_=bias_sorted_t[:, :, 0])
 
+        signs = const.tile([P, HEAD_DIM], BF16, name="signs")
+        nc.vector.memset(signs[:], 1.0)
+        nc.vector.memset(signs[:].rearrange("p (i e) -> p i e", e=2)[:, :, 0], -1.0)
+
         def sign_sin(first, last):
-            even = sin_sb[:, first:last, :].rearrange("p m (i e) -> p m i e", e=2)[:, :, :, 0]
-            nc.scalar.mul(out=even, in_=even, mul=-1.0)
+            nc.vector.tensor_tensor(
+                out=sin_sb[:, first:last, :],
+                in0=sin_sb[:, first:last, :],
+                in1=signs[:].unsqueeze(1).to_broadcast([P, last - first, HEAD_DIM]),
+                op=MULT,
+            )
 
         def transpose_round(r):
             grouped = mx_pool.tile([P, PASSES, ROUND, P, PACK], BF16, name="grouped", align_bytes=64)

from contextlib import ExitStack

import concourse.mybir as mybir
from concourse.masks import make_identity

F32 = mybir.dt.float32
BF16 = mybir.dt.bfloat16
U32 = mybir.dt.uint32
U8 = mybir.dt.uint8
FP8X4 = mybir.dt.float8_e4m3fn_x4
MULT = mybir.AluOpType.mult
ADD = mybir.AluOpType.add
IDENTITY = mybir.ActivationFunctionType.Identity

P = 128
PACK = 4
TOKENS = 8192
HIDDEN = 1024
HEAD_DIM = 32
PAIRS = HEAD_DIM // 2
QK_HEADS = 8
QK = QK_HEADS * HEAD_DIM
HALF = QK // 2
V = 4 * HEAD_DIM
BANK = 512
PASSES = HIDDEN // (P * PACK)
WORD_BLOCKS = HIDDEN // (2 * P)
TILES = TOKENS // P
ROUND = 2
ROUNDS = TILES // ROUND
BLOCK = 4
BLOCKS = TILES // BLOCK
X_BUFS = 3
TABLE_PARTS = {0: 16, 16: TILES}

FLOPS = 2 * TOKENS * HIDDEN * (QK + V)


def tile_arlowvisionattention_pa_t_kernel(
    tc, hidden_states, cos, sin, w_qkv, b_qkv, out_0, out_1, out_2
):
    nc = tc.nc
    x_view = hidden_states.rearrange("(p m) k -> p m k", m=TILES)
    out_views = [o.rearrange("(p m) h d -> p m (h d)", m=TILES) for o in (out_0, out_1, out_2)]

    with ExitStack() as ctx:
        const = ctx.enter_context(tc.tile_pool(name="const", bufs=1))
        x_pool = ctx.enter_context(tc.tile_pool(name="x", bufs=X_BUFS))
        mx_pool = ctx.enter_context(tc.tile_pool(name="mx", bufs=3))
        rope_pool = ctx.enter_context(tc.tile_pool(name="rope", bufs=3))
        out_pool = ctx.enter_context(tc.tile_pool(name="out", bufs=3))
        psum_x = ctx.enter_context(tc.psum_pool(name="psum_x", bufs=2))
        psum_qk_t = ctx.enter_context(tc.psum_pool(name="psum_qk_t", bufs=2))
        psum_qk = ctx.enter_context(tc.psum_pool(name="psum_qk", bufs=2))
        psum_v = ctx.enter_context(tc.psum_pool(name="psum_v", bufs=2))
        ctx.enter_context(tc.manual_schedule())

        x_blocks = {}

        def load_tiles(first, count):
            b = first // BLOCK
            if first % BLOCK == 0:
                x_blocks[b] = x_pool.tile([P, BLOCK, HIDDEN], BF16, name="x_blk")
            nc.sync.dma_start(
                out=x_blocks[b][:, first % BLOCK : first % BLOCK + count, :],
                in_=x_view[:, first : first + count, :],
            )

        cos_sb = const.tile([P, TILES, HEAD_DIM], BF16, name="cos_sb")
        sin_sb = const.tile([P, TILES, HEAD_DIM], BF16, name="sin_sb")

        def load_tables(first, last):
            for table_sb, table in ((cos_sb, cos), (sin_sb, sin)):
                nc.sync.dma_start(
                    out=table_sb[:, first:last, :],
                    in_=table.rearrange("(p m) d -> p m d", m=TILES)[:, first:last, :],
                )

        bias_row = const.tile([P, BANK], BF16, name="bias_row")
        nc.vector.memset(bias_row[:], 0.0)
        nc.sync.dma_start(out=bias_row[0:1, 0 : QK + V], in_=b_qkv.rearrange("(o n) -> o n", o=1))
        load_tiles(0, ROUND)
        w_raw = const.tile([P, PASSES * 2, 2, QK + V], BF16, name="w_raw")
        nc.sync.dma_start(
            out=w_raw[:], in_=w_qkv.rearrange("(gu p e) c -> p gu e c", gu=PASSES * 2, e=2)
        )
        load_tiles(ROUND, ROUND)
        load_tables(0, TABLE_PARTS[0])
        for first in range(BLOCK, X_BUFS * BLOCK, ROUND):
            load_tiles(first, ROUND)
        load_tables(TABLE_PARTS[0], TILES)

        ident_f32 = const.tile([P, P], F32, name="ident_f32")
        make_identity(nc, ident_f32[:])
        ident_bf16 = const.tile([P, P], BF16, name="ident_bf16")
        make_identity(nc, ident_bf16[:])

        ones = const.tile([P, P], BF16, name="ones")
        nc.vector.memset(ones[:], 1.0)
        bias_spread = psum_qk.tile([P, BANK], F32, name="bias_spread", tag="qk")
        nc.tensor.matmul(out=bias_spread[:], lhsT=ones[:], rhs=bias_row[:], start=True, stop=True)
        bias_v = const.tile([P, V], BF16, name="bias_v")
        nc.scalar.copy(out=bias_v[:], in_=bias_spread[:, QK : QK + V])
        bias_sorted = const.tile([P, 2, HALF], BF16, name="bias_sorted")
        nc.vector.tensor_copy(
            out=bias_sorted[:], in_=bias_row[:, 0:QK].rearrange("p (n e) -> p e n", e=2)
        )
        bias_sorted_t = psum_x.tile([P, 2, P], BF16, name="bias_sorted_t", tag="x_t")
        for e in range(2):
            nc.tensor.transpose(bias_sorted_t[:, e, :], bias_sorted[:, e, :], ident_bf16[:])
        bias_qk = const.tile([P, 2], F32, name="bias_qk")
        nc.scalar.copy(out=bias_qk[:], in_=bias_sorted_t[:, :, 0])

        signs = const.tile([P, HEAD_DIM], BF16, name="signs")
        nc.vector.memset(signs[:], 1.0)
        nc.vector.memset(signs[:].rearrange("p (i e) -> p i e", e=2)[:, :, 0], -1.0)

        def sign_sin(first, last):
            nc.vector.tensor_tensor(
                out=sin_sb[:, first:last, :],
                in0=sin_sb[:, first:last, :],
                in1=signs[:].unsqueeze(1).to_broadcast([P, last - first, HEAD_DIM]),
                op=MULT,
            )

        def transpose_round(r):
            grouped = mx_pool.tile([P, PASSES, ROUND, P, PACK], BF16, name="grouped", align_bytes=64)
            grouped_words = grouped[:].bitcast(F32)
            for a in range(ROUND):
                tile_in_block = (r * ROUND + a) % BLOCK
                words = x_blocks[r * ROUND // BLOCK][:, tile_in_block, :].bitcast(F32)
                x_t = psum_x.tile([P, WORD_BLOCKS, P], F32, name="x_t", tag="x_t")
                for j in range(WORD_BLOCKS):
                    nc.tensor.transpose(x_t[:, j, :], words[:, j * P : (j + 1) * P], ident_f32[:])
                nc.scalar.copy(
                    out=grouped_words[:, :, a], in_=x_t[:].rearrange("p (g u) r -> p g r u", u=2)
                )
            if (r + 1) * ROUND % BLOCK == 0 and r * ROUND // BLOCK + X_BUFS < BLOCKS:
                load_tiles((r * ROUND // BLOCK + X_BUFS) * BLOCK, BLOCK)
            return grouped

        def quantise_round(grouped):
            codes = mx_pool.tile([P, PASSES, ROUND, P], U32, name="codes", align_bytes=64)
            scales = mx_pool.tile([P, PASSES, ROUND, P], U8, name="scales", align_bytes=64)
            nc.vector.quantize_mx(
                out=codes[:].rearrange("p g a r -> p (g a r)").bitcast(FP8X4),
                scales=scales[:].rearrange("p g a r -> p (g a r)"),
                in_=grouped[:].rearrange("p g a r t -> p (g a r t)"),
            )
            return codes, scales

        def project_round(codes_and_scales):
            codes, scales = codes_and_scales
            qk_t = psum_qk_t.tile([P, 2, ROUND * P], F32, name="qk_t")
            for e in range(2):
                for g in range(PASSES):
                    nc.tensor.matmul_mx(
                        out=qk_t[:, e, :],
                        lhsT=w_qk_codes[:, g, e, :].bitcast(FP8X4),
                        lhsT_scale=w_qk_scales[:, g, e, :],
                        rhs=codes[:, g].rearrange("p a r -> p (a r)").bitcast(FP8X4),
                        rhs_scale=scales[:, g].rearrange("p a r -> p (a r)"),
                        start=(g == 0),
                        stop=(g == PASSES - 1),
                    )
            v = psum_v.tile([P, ROUND, V], F32, name="v")
            for a in range(ROUND):
                for g in range(PASSES):
                    nc.tensor.matmul_mx(
                        out=v[:, a, :],
                        lhsT=codes[:, g, a, :].bitcast(FP8X4),
                        lhsT_scale=scales[:, g, a, :],
                        rhs=w_v_codes[:, g, :].bitcast(FP8X4),
                        rhs_scale=w_v_scales[:, g, :],
                        start=(g == 0),
                        stop=(g == PASSES - 1),
                    )
            qk_t_sb = rope_pool.tile([P, 2, ROUND * P], F32, name="qk_t_sb")
            for e in range(2):
                nc.scalar.activation(
                    out=qk_t_sb[:, e, :],
                    in_=qk_t[:, e, :],
                    func=IDENTITY,
                    bias=bias_qk[:, e : e + 1],
                    scale=1.0,
                )
            return qk_t_sb, v

        def turn_back_round(qk_t_sb):
            qk = psum_qk.tile([P, ROUND, 2, HALF], F32, name="qk", tag="qk")
            for a in range(ROUND):
                for e in range(2):
                    nc.tensor.transpose(
                        qk[:, a, e, :], qk_t_sb[:, e, a * P : (a + 1) * P], ident_f32[:]
                    )
            return qk

        def multiply_round(r, qk):
            shape = [P, ROUND, QK_HEADS, PAIRS, 2]
            tiles = slice(r * ROUND, (r + 1) * ROUND)
            halves = qk[:].rearrange("p a e (h i) -> p a e h i", i=PAIRS)
            by_cos = rope_pool.tile(shape, F32, name="by_cos")
            nc.vector.tensor_tensor(
                out=by_cos[:],
                in0=halves.rearrange("p a e h i -> p a h i e"),
                in1=cos_sb[:, tiles, :].rearrange("p a (i e) -> p a i e", e=2).unsqueeze(2).to_broadcast(shape),
                op=MULT,
            )
            by_sin = rope_pool.tile(shape, F32, name="by_sin")
            nc.vector.tensor_tensor(
                out=by_sin[:],
                in0=halves[:, :, ::-1].rearrange("p a e h i -> p a h i e"),
                in1=sin_sb[:, tiles, :].rearrange("p a (i e) -> p a i e", e=2).unsqueeze(2).to_broadcast(shape),
                op=MULT,
            )
            return by_cos, by_sin

        def finish_qk_round(r, by_cos, by_sin, out_blk):
            first = r * ROUND % BLOCK
            nc.gpsimd.tensor_tensor(
                out=out_blk[:, 0:2, first : first + ROUND, :],
                in0=by_cos[:].rearrange("p a (j h) i e -> p j a (h i e)", j=2),
                in1=by_sin[:].rearrange("p a (j h) i e -> p j a (h i e)", j=2),
                op=ADD,
            )

        def finish_v_round(r, v, out_blk):
            first = r * ROUND % BLOCK
            nc.vector.tensor_tensor(
                out=out_blk[:, 2, first : first + ROUND, :],
                in0=v[:],
                in1=bias_v[:].unsqueeze(1).to_broadcast([P, ROUND, V]),
                op=ADD,
            )

        def store_tiles(out_blk, first, count):
            for j in range(3):
                nc.sync.dma_start(
                    out=out_views[j][:, first : first + count, :],
                    in_=out_blk[:, j, first % BLOCK : first % BLOCK + count, :],
                )

        quantised = {0: quantise_round(transpose_round(0))}

        w_rows = w_raw[:].rearrange("p (g u) e c -> p g (u e) c", u=2)
        w_halves = w_rows[:, :, :, 0:QK].rearrange("p g t (n e) -> p e g n t", e=2)
        w_qk_grouped = const.tile([P, PASSES, 2, HALF, PACK], BF16, name="w_qk_grouped", align_bytes=64)
        nc.vector.tensor_copy(out=w_qk_grouped[:, :, 0], in_=w_halves[:, 0])
        nc.scalar.copy(out=w_qk_grouped[:, :, 1], in_=w_halves[:, 1])
        w_qk_codes = const.tile([P, PASSES, 2, HALF], U32, name="w_qk_codes", align_bytes=64)
        w_qk_scales = const.tile([P, PASSES, 2, HALF], U8, name="w_qk_scales", align_bytes=64)
        nc.vector.quantize_mx(
            out=w_qk_codes[:].rearrange("p g e n -> p (g e n)").bitcast(FP8X4),
            scales=w_qk_scales[:].rearrange("p g e n -> p (g e n)"),
            in_=w_qk_grouped[:].rearrange("p g e n t -> p (g e n t)"),
        )
        w_v_grouped = const.tile([P, PASSES, V, PACK], BF16, name="w_v_grouped", align_bytes=64)
        nc.vector.tensor_copy(
            out=w_v_grouped[:], in_=w_rows[:, :, :, QK : QK + V].rearrange("p g t n -> p g n t")
        )
        w_v_codes = const.tile([P, PASSES, V], U32, name="w_v_codes", align_bytes=64)
        w_v_scales = const.tile([P, PASSES, V], U8, name="w_v_scales", align_bytes=64)
        nc.vector.quantize_mx(
            out=w_v_codes[:].rearrange("p g n -> p (g n)").bitcast(FP8X4),
            scales=w_v_scales[:].rearrange("p g n -> p (g n)"),
            in_=w_v_grouped[:].rearrange("p g n t -> p (g n t)"),
        )

        projected, turned_back, out_blks = {}, {}, {}
        for r in range(-2, ROUNDS):
            grouped = None
            if r + 3 < ROUNDS:
                grouped = transpose_round(r + 3)
            if 0 <= r + 1 < ROUNDS:
                turned_back[r + 1] = turn_back_round(projected[r + 1][0])
            if 0 <= r + 2 < ROUNDS:
                projected[r + 2] = project_round(quantised[r + 2])
            if (r + 1) * ROUND in TABLE_PARTS:
                sign_sin((r + 1) * ROUND, TABLE_PARTS[(r + 1) * ROUND])
            if r >= 0:
                by_cos, by_sin = multiply_round(r, turned_back[r])
            if r + 3 < ROUNDS:
                quantised[r + 3] = quantise_round(grouped)
            if 0 <= r + 1 < ROUNDS:
                if (r + 1) * ROUND % BLOCK == 0:
                    out_blks[(r + 1) * ROUND // BLOCK] = out_pool.tile(
                        [P, 3, BLOCK, V], F32, name="out_blk"
                    )
                finish_v_round(r + 1, projected[r + 1][1], out_blks[(r + 1) * ROUND // BLOCK])
            if r >= 0:
                b = r * ROUND // BLOCK
                finish_qk_round(r, by_cos, by_sin, out_blks[b])
                if b == BLOCKS - 1:
                    store_tiles(out_blks[b], r * ROUND, ROUND)
                elif (r + 1) * ROUND % BLOCK == 0:
                    store_tiles(out_blks[b], b * BLOCK, BLOCK)
